import numpy as np
import ml_dtypes


def mxq(x, axis, fmt="e4m3"):
    dtype, down = {"e4m3": (ml_dtypes.float8_e4m3fn, 7), "e5m2": (ml_dtypes.float8_e5m2, 14)}[fmt]
    v = np.moveaxis(np.asarray(x, np.float32).astype(ml_dtypes.bfloat16).astype(np.float64), axis, -1)
    blocks = v.reshape(v.shape[:-1] + (-1, 32))
    amax = np.abs(blocks).max(-1, keepdims=True)
    byte = np.maximum(np.where(amax > 0, np.frexp(amax)[1] - 1 + 127, 0) - down, 1)
    scale = np.exp2(byte - 127.0)
    codes = (blocks / scale).astype(np.float32).astype(dtype).astype(np.float64)
    return np.moveaxis((codes * scale).reshape(v.shape), -1, axis)


WIDE = False


def mx_kscale(k):
    if not WIDE:
        return np.ones(k)
    levels = np.array([10, -10, 5, -5, 0])
    if k % 512:
        return np.exp2(np.random.permutation(np.resize(levels, k // 32))).repeat(32)
    a = np.empty((k // 512, 16))
    for p in range(k // 512):
        a[p, :8] = np.random.permutation(np.resize(levels, 8))
        for g in range(8):
            far = levels[np.abs(levels - a[p, g]) >= 10]
            a[p, g + 8] = far[np.random.randint(len(far))]
    return np.exp2(a.ravel()).repeat(32)


BF16 = ml_dtypes.bfloat16


def bf(x):
    return np.asarray(x, np.float32).astype(BF16)


def f64(x):
    return np.asarray(x).astype(np.float64)


B, N, E, L, A, H1, H2, G = 1024, 8, 8, 384, 128, 512, 1024, 8
D = L + A
EPS = 1e-5


def mish(v):
    return v * np.tanh(np.log(1.0 + np.exp(v)))


def layer_norm(v, gamma, beta):
    mu = v.mean(-1, keepdims=True)
    var = v.var(-1, keepdims=True)
    return (v - mu) / np.sqrt(var + EPS) * gamma + beta


def setup_inputs():
    s = mx_kscale(D)
    r = np.random.standard_normal
    return {"tokens": bf(r((B, N, D)) * s),
            "logits": bf(r((B, N, E))),
            "W1": bf(r((E, D, H1)) / np.sqrt(D) / s[:, None]),
            "b1": bf(0.1 * r((E, H1))),
            "g1": bf(1.0 + 0.1 * r((E, H1))),
            "be1": bf(0.1 * r((E, H1)))}


def reference(tokens, logits, W1, b1, g1, be1):
    tok, lg = f64(tokens), f64(logits)
    ex = np.exp(lg - lg.max(1, keepdims=True))
    disp = ex / ex.sum(1, keepdims=True)
    slot = sum(disp[:, n, :].T[:, :, None] * tok[None, :, n, :] for n in range(N))
    h = (mxq(slot, 2, "e4m3") @ mxq(f64(W1), 1, "e4m3")) + f64(b1)[:, None, :]
    h = mish(layer_norm(h, f64(g1)[:, None, :], f64(be1)[:, None, :]))
    return h.transpose(1, 0, 2)

@@ -1,0 +1,319 @@
+from contextlib import ExitStack
+
+import concourse.mybir as mybir
+from concourse.masks import make_identity
+
+F32 = mybir.dt.float32
+BF16 = mybir.dt.bfloat16
+U32 = mybir.dt.uint32
+U8 = mybir.dt.uint8
+FP8X4 = mybir.dt.float8_e4m3fn_x4
+ALU = mybir.AluOpType
+ACT = mybir.ActivationFunctionType
+AX = mybir.AxisListType
+
+P = 128
+B, AGENTS, E, K, H = 1024, 8, 8, 512, 512
+TILES = B // P
+PACK = 4
+GROUP = P // AGENTS
+GROUPS = P // GROUP
+EPS = 1e-5
+FLOPS = 2 * B * E * K * H + 2 * B * E * AGENTS * K
+
+BLOCK_TILES = (0, 2, 4)
+PARTS = 4
+ON_SCALAR = 2
+HALVES = (slice(0, E * H // 2), slice(E * H // 2, E * H))
+
+
+def tile_softmoedynamics_pa_t_kernel(tc, tokens, logits, W1, b1, g1, be1, out):
+    nc = tc.nc
+    with ExitStack() as ctx:
+        const = ctx.enter_context(tc.tile_pool(name="const", bufs=1))
+        tok_pool = ctx.enter_context(tc.tile_pool(name="tok_pool", bufs=2))
+        group_pool = ctx.enter_context(tc.tile_pool(name="group_pool", bufs=2))
+        diag_pool = ctx.enter_context(tc.tile_pool(name="diag_pool", bufs=1))
+        sum_pool = ctx.enter_context(tc.tile_pool(name="sum_pool", bufs=3))
+        slot_pool = ctx.enter_context(tc.tile_pool(name="slot_pool", bufs=1))
+        code_pool = ctx.enter_context(tc.tile_pool(name="code_pool", bufs=2))
+        x_pool = ctx.enter_context(tc.tile_pool(name="x_pool", bufs=1))
+        v_pool = ctx.enter_context(tc.tile_pool(name="v_pool", bufs=2))
+        small = ctx.enter_context(tc.tile_pool(name="small", bufs=2))
+        slot_banks = ctx.enter_context(tc.psum_pool(name="slot_banks", bufs=4))
+        layer_banks = ctx.enter_context(tc.psum_pool(name="layer_banks", bufs=4))
+
+        identity = const.tile([P, P], F32)
+        make_identity(nc, identity[:])
+        same_batch = const.tile([P, GROUP], F32)
+        nc.vector.tensor_reduce(
+            out=same_batch[:], in_=identity[:].rearrange("p (g c) -> p c g", c=GROUP), axis=AX.X, op=ALU.add
+        )
+        minus_half = const.tile([P, E], F32)
+        nc.vector.memset(minus_half[:], -0.5)
+
+        bias_rows = const.tile([P, E * H], BF16)
+        gain_rows = const.tile([P, E * H], BF16)
+        shift_rows = const.tile([P, E * H], BF16)
+        disp = const.tile([P, TILES, AGENTS, E], F32)
+        w_codes = const.tile([P, E, H], U32, align_bytes=64)
+        w_scales = const.tile([P, E, H], U8, align_bytes=64)
+
+        def softmax_over_agents(pool):
+            shape = [P, TILES, AGENTS, E]
+            raw = pool.tile(shape, BF16)
+            nc.sync.dma_start(out=raw[:], in_=logits.rearrange("(t p) n e -> p t n e", p=P))
+            top = pool.tile([P, TILES, E], F32)
+            nc.vector.tensor_reduce(out=top[:], in_=raw[:].rearrange("p t n e -> p t e n"), axis=AX.X, op=ALU.max)
+            ex = pool.tile(shape, F32)
+            nc.vector.tensor_tensor(out=ex[:], in0=raw[:], in1=top[:].unsqueeze(2).to_broadcast(shape), op=ALU.subtract)
+            flat = ex[:].rearrange("p t n e -> p (t n e)")
+            nc.scalar.activation(out=flat, in_=flat, func=ACT.Exp)
+            total = pool.tile([P, TILES, E], F32)
+            nc.vector.tensor_reduce(out=total[:], in_=ex[:].rearrange("p t n e -> p t e n"), axis=AX.X, op=ALU.add)
+            inverse = pool.tile([P, TILES, E], F32)
+            nc.vector.reciprocal(out=inverse[:], in_=total[:])
+            nc.vector.tensor_tensor(
+                out=disp[:], in0=ex[:], in1=inverse[:].unsqueeze(2).to_broadcast(shape), op=ALU.mult
+            )
+
+        def quantise_weights(e, pool):
+            rows = pool.tile([P, PACK, H], BF16)
+            nc.sync.dma_start(out=rows[:], in_=W1[e].rearrange("(p t) h -> p t h", t=PACK))
+            words = pool.tile([P, H, PACK], BF16, align_bytes=64)
+            dst = words[:].rearrange("p (c i) t -> p c t i", i=4)
+            src = rows[:].rearrange("p t (c i) -> p c t i", i=4)
+            if e % 2 == 1:
+                nc.vector.tensor_copy(out=dst, in_=src)
+            else:
+                nc.scalar.copy(out=dst, in_=src)
+            nc.vector.quantize_mx(
+                out=w_codes[:, e, :].bitcast(FP8X4),
+                scales=w_scales[:, e, :],
+                in_=words[:].rearrange("p h t -> p (h t)"),
+            )
+
+        product_tiles = [bt for bt in range(TILES) if bt not in BLOCK_TILES]
+        made = {"product": 0, "block": 0}
+        current = {}
+        slot_codes = {}
+
+        def quantise_slots(bt, words):
+            codes = code_pool.tile([P, E * P], U32, align_bytes=64)
+            scales = code_pool.tile([P, E * P], U8, align_bytes=64)
+            nc.vector.quantize_mx(
+                out=codes[:].bitcast(FP8X4), scales=scales[:], in_=words[:].rearrange("p e b t -> p (e b t)")
+            )
+            slot_codes[bt] = (codes, scales)
+
+        def product_unit():
+            unit = made["product"]
+            if unit == E * len(product_tiles):
+                return
+            made["product"] = unit + 1
+            bt, e = product_tiles[unit // E], unit % E
+            if e == 0:
+                tok = tok_pool.tile([P, AGENTS, K], BF16)
+                nc.sync.dma_start(out=tok[:], in_=tokens[bt * P : (bt + 1) * P])
+                words = slot_pool.tile([P, E, P, PACK], BF16, align_bytes=64, tag="product_words")
+                current["product"] = (tok, words)
+            tok, words = current["product"]
+            parts, on_scalar = PARTS, ON_SCALAR
+            sums = sum_pool.tile([P, parts, K], F32, tag="sums")
+            length = AGENTS // parts
+            by_word = lambda row: row.rearrange("b (p t) -> b t p", t=PACK)
+            for r in range(length):
+                for q in range(parts):
+                    n = q * length + r
+                    weight = disp[:, bt, n, e : e + 1]
+                    target = sums[:, q, :].rearrange("b (t p) -> b t p", t=PACK)
+                    if r > 0:
+                        nc.vector.scalar_tensor_tensor(
+                            out=target, in0=by_word(tok[:, n, :]), scalar=weight, in1=target,
+                            op0=ALU.mult, op1=ALU.add,
+                        )
+                    elif q < on_scalar:
+                        nc.scalar.activation(out=target, in_=by_word(tok[:, n, :]), func=ACT.Copy, scale=weight)
+                    else:
+                        nc.vector.tensor_scalar(
+                            out=target, in0=by_word(tok[:, n, :]), scalar1=weight, scalar2=None, op0=ALU.mult
+                        )
+            bank = slot_banks.tile([P, PACK, P], F32, tag="bank")
+            for t in range(PACK):
+                for q in range(parts):
+                    nc.tensor.matmul(
+                        bank[:, t, :], lhsT=sums[:, q, t * P : (t + 1) * P], rhs=identity[:],
+                        is_transpose=True, start=(q == 0), stop=(q == parts - 1),
+                    )
+            nc.scalar.copy(out=words[:, e], in_=bank[:].rearrange("p t b -> p b t"))
+            if e == E - 1:
+                quantise_slots(bt, words)
+
+        def block_unit():
+            unit = made["block"]
+            if unit == GROUPS * len(BLOCK_TILES):
+                return
+            made["block"] = unit + 1
+            bt, g = BLOCK_TILES[unit // GROUPS], unit % GROUPS
+            if g == 0:
+                shape = [P, E, GROUP, AGENTS]
+                spread = sum_pool.tile(shape, F32, tag="sums")
+                nc.vector.tensor_tensor(
+                    out=spread[:],
+                    in0=disp[:, bt].rearrange("p n e -> p e n").unsqueeze(2).to_broadcast(shape),
+                    in1=same_batch[:].unsqueeze(1).unsqueeze(3).to_broadcast(shape),
+                    op=ALU.mult,
+                )
+                diag = diag_pool.tile([P, GROUPS, E, GROUP], F32)
+                for half in range(2):
+                    bank = slot_banks.tile([P, PACK, P], F32, tag="bank")
+                    for i in range(PACK):
+                        nc.tensor.transpose(
+                            bank[:, i, :], spread[:, half * PACK + i].rearrange("p c n -> p (c n)"), identity[:]
+                        )
+                    nc.scalar.copy(
+                        out=diag[:, :, half * PACK : (half + 1) * PACK, :],
+                        in_=bank[:].rearrange("p e (g c) -> p g e c", c=GROUP),
+                    )
+                words = slot_pool.tile([P, E, P, PACK], BF16, align_bytes=64, tag="block_words")
+                current["block"] = (diag, words)
+            diag, words = current["block"]
+            tok = group_pool.tile([P, K], BF16)
+            first = bt * P + g * GROUP
+            nc.sync.dma_start(out=tok[:], in_=tokens[first : first + GROUP].rearrange("b n k -> (b n) k"))
+            tok32 = group_pool.tile([P, K], F32)
+            nc.scalar.copy(
+                out=tok32[:].rearrange("r (t p) -> r t p", t=PACK), in_=tok[:].rearrange("r (p t) -> r t p", t=PACK)
+            )
+            bank = slot_banks.tile([P, PACK, P], F32, tag="bank")
+            for t in range(PACK):
+                nc.tensor.matmul(
+                    bank[:, t, :], lhsT=tok32[:, t * P : (t + 1) * P], rhs=diag[:, g].rearrange("p e c -> p (e c)"),
+                    start=True, stop=True,
+                )
+            nc.scalar.copy(
+                out=words[:, :, g * GROUP : (g + 1) * GROUP, :],
+                in_=bank[:].rearrange("p t (e c) -> p e c t", c=GROUP),
+            )
+            if g == GROUPS - 1:
+                quantise_slots(bt, words)
+
+        work = {}
+
+        def layer_and_centre(bt):
+            if bt == TILES:
+                return
+            codes, scales = slot_codes[bt]
+            x = x_pool.tile([P, E, H], F32)
+            v = v_pool.tile([P, E, H], F32)
+            total = small.tile([P, E], F32)
+            minus_mean = small.tile([P, E], F32)
+            squares = small.tile([P, E], F32)
+            for e in range(E):
+                bank = layer_banks.tile([P, H], F32)
+                nc.tensor.matmul_mx(
+                    out=bank[:],
+                    lhsT=codes[:, e * P : (e + 1) * P].bitcast(FP8X4),
+                    lhsT_scale=scales[:, e * P : (e + 1) * P],
+                    rhs=w_codes[:, e, :].bitcast(FP8X4),
+                    rhs_scale=w_scales[:, e, :],
+                    start=True,
+                    stop=True,
+                )
+                nc.vector.scalar_tensor_tensor(
+                    out=x[:, e, :], in0=bank[:], scalar=1.0, in1=bias_rows[:, e * H : (e + 1) * H],
+                    op0=ALU.mult, op1=ALU.add, accum_out=total[:, e : e + 1],
+                )
+            nc.vector.tensor_scalar(out=minus_mean[:], in0=total[:], scalar1=-1.0 / H, scalar2=None, op0=ALU.mult)
+            for e in range(E):
+                unused = small.tile([P, H], BF16)
+                nc.scalar.activation(
+                    out=unused[:], in_=x[:, e, :], func=ACT.Square, bias=minus_mean[:, e : e + 1], scale=1.0,
+                    accum_out=squares[:, e : e + 1],
+                )
+                nc.vector.scalar_tensor_tensor(
+                    out=v[:, e, :], in0=x[:, e, :], scalar=minus_mean[:, e : e + 1],
+                    in1=gain_rows[:, e * H : (e + 1) * H], op0=ALU.add, op1=ALU.mult,
+                )
+            work[bt] = {"v": v, "squares": squares}
+
+        def inverse_std(bt):
+            if bt == TILES:
+                return
+            variance = small.tile([P, E], F32)
+            inverse = small.tile([P, E], F32)
+            nc.vector.tensor_scalar(
+                out=variance[:], in0=work[bt]["squares"][:], scalar1=1.0 / H, scalar2=EPS, op0=ALU.mult, op1=ALU.add
+            )
+            nc.gpsimd.tensor_tensor(out=inverse[:], in0=variance[:], in1=minus_half[:], op=ALU.pow)
+            work[bt]["inverse"] = inverse
+
+        def scale_and_shift(bt):
+            if bt == TILES:
+                return
+            v, inverse = work[bt]["v"], work[bt]["inverse"]
+            for e in range(E):
+                nc.vector.scalar_tensor_tensor(
+                    out=v[:, e, :], in0=v[:, e, :], scalar=inverse[:, e : e + 1],
+                    in1=shift_rows[:, e * H : (e + 1) * H], op0=ALU.mult, op1=ALU.add,
+                )
+
+        def mish_exp(bt, pool):
+            if bt < 0:
+                return
+            u = pool.tile([P, E * H], F32)
+            work[bt]["u"] = u
+            v = work[bt]["v"][:].rearrange("p e h -> p (e h)")
+            for cols in HALVES:
+                nc.scalar.activation(out=u[:, cols], in_=v[:, cols], func=ACT.Exp)
+
+        def mish_log(bt):
+            if bt < 0:
+                return
+            u = work[bt]["u"]
+            for cols in HALVES:
+                nc.scalar.activation(out=u[:, cols], in_=u[:, cols], func=ACT.Ln, bias=1.0, scale=1.0)
+
+        def mish_tanh(bt):
+            if bt < 0:
+                return
+            u = work[bt]["u"]
+            for cols in HALVES:
+                nc.scalar.activation(out=u[:, cols], in_=u[:, cols], func=ACT.Tanh)
+
+        def multiply_and_store(bt):
+            if bt < 0:
+                return
+            u = work[bt]["u"]
+            v = work[bt]["v"][:].rearrange("p e h -> p (e h)")
+            rows = out[bt * P : (bt + 1) * P].rearrange("b e h -> b (e h)")
+            for cols in HALVES:
+                nc.vector.tensor_tensor(out=u[:, cols], in0=v[:, cols], in1=u[:, cols], op=ALU.mult)
+                nc.sync.dma_start(out=rows[:, cols], in_=u[:, cols])
+
+        with tc.tile_pool(name="early", bufs=1) as early, tc.tile_pool(name="staging", bufs=2) as staging:
+            softmax_over_agents(early)
+            for e in range(E):
+                block_unit()
+                product_unit()
+                quantise_weights(e, staging)
+            for rows, vector in ((bias_rows, b1), (gain_rows, g1), (shift_rows, be1)):
+                nc.sync.dma_start(out=rows[:], in_=vector.rearrange("e h -> (e h)").partition_broadcast(P))
+        mish_pool = ctx.enter_context(tc.tile_pool(name="mish_pool", bufs=2))
+        for j in range(-1, TILES):
+            mish_exp(j, mish_pool)
+            layer_and_centre(j + 1)
+            product_unit()
+            inverse_std(j + 1)
+            block_unit()
+            mish_log(j)
+            product_unit()
+            block_unit()
+            scale_and_shift(j + 1)
+            mish_tanh(j)
+            product_unit()
+            block_unit()
+            multiply_and_store(j)
+            product_unit()
+            block_unit()
+            product_unit()

@@ -22,8 +22,8 @@ EPS = 1e-5
 FLOPS = 2 * B * E * K * H + 2 * B * E * AGENTS * K
 
 BLOCK_TILES = (0, 2, 4)
-PARTS = 4
-ON_SCALAR = 2
+PARTS = 8
+ON_SCALAR = 1
 HALVES = (slice(0, E * H // 2), slice(E * H // 2, E * H))
 
 

@@ -21,10 +21,12 @@ GROUPS = P // GROUP
 EPS = 1e-5
 FLOPS = 2 * B * E * K * H + 2 * B * E * AGENTS * K
 
-BLOCK_TILES = (0, 2, 4)
-PARTS = 8
-ON_SCALAR = 1
-HALVES = (slice(0, E * H // 2), slice(E * H // 2, E * H))
+BLOCK_TILES = (2, 4, 6)
+HALF = E // 2
+CHUNKS = 2 * TILES
+MISH_GROUPS = (2, 4, 4, 4, 1, 1)
+PRODUCTS_AT = {1: (0, 1, 2, 3), 2: (0, 1, 2, 3)}
+BLOCKS_AT = {1: (1, 2, 3), 2: (0, 1, 2, 3)}
 
 
 def tile_softmoedynamics_pa_t_kernel(tc, tokens, logits, W1, b1, g1, be1, out):
@@ -32,25 +34,21 @@ def tile_softmoedynamics_pa_t_kernel(tc, tokens, logits, W1, b1, g1, be1, out):
     with ExitStack() as ctx:
         const = ctx.enter_context(tc.tile_pool(name="const", bufs=1))
         tok_pool = ctx.enter_context(tc.tile_pool(name="tok_pool", bufs=2))
-        group_pool = ctx.enter_context(tc.tile_pool(name="group_pool", bufs=2))
+        group_pool = ctx.enter_context(tc.tile_pool(name="group_pool", bufs=3))
         diag_pool = ctx.enter_context(tc.tile_pool(name="diag_pool", bufs=1))
-        sum_pool = ctx.enter_context(tc.tile_pool(name="sum_pool", bufs=3))
-        slot_pool = ctx.enter_context(tc.tile_pool(name="slot_pool", bufs=1))
-        code_pool = ctx.enter_context(tc.tile_pool(name="code_pool", bufs=2))
-        x_pool = ctx.enter_context(tc.tile_pool(name="x_pool", bufs=1))
-        v_pool = ctx.enter_context(tc.tile_pool(name="v_pool", bufs=2))
-        small = ctx.enter_context(tc.tile_pool(name="small", bufs=2))
+        sum_pool = ctx.enter_context(tc.tile_pool(name="sum_pool", bufs=7))
+        slot_pool = ctx.enter_context(tc.tile_pool(name="slot_pool", bufs=3))
+        block_pool = ctx.enter_context(tc.tile_pool(name="block_pool", bufs=1))
+        code_pool = ctx.enter_context(tc.tile_pool(name="code_pool", bufs=3))
+        v_pool = ctx.enter_context(tc.tile_pool(name="v_pool", bufs=7))
+        small = ctx.enter_context(tc.tile_pool(name="small", bufs=3))
         slot_banks = ctx.enter_context(tc.psum_pool(name="slot_banks", bufs=4))
         layer_banks = ctx.enter_context(tc.psum_pool(name="layer_banks", bufs=4))
 
-        identity = const.tile([P, P], F32)
-        make_identity(nc, identity[:])
-        same_batch = const.tile([P, GROUP], F32)
-        nc.vector.tensor_reduce(
-            out=same_batch[:], in_=identity[:].rearrange("p (g c) -> p c g", c=GROUP), axis=AX.X, op=ALU.add
-        )
-        minus_half = const.tile([P, E], F32)
+        minus_half = const.tile([P, HALF], F32)
         nc.vector.memset(minus_half[:], -0.5)
+        warm = const.tile([P, HALF], F32)
+        nc.scalar.activation(out=warm[:], in_=minus_half[:], func=ACT.Exp)
 
         bias_rows = const.tile([P, E * H], BF16)
         gain_rows = const.tile([P, E * H], BF16)
@@ -58,96 +56,166 @@ def tile_softmoedynamics_pa_t_kernel(tc, tokens, logits, W1, b1, g1, be1, out):
         disp = const.tile([P, TILES, AGENTS, E], F32)
         w_codes = const.tile([P, E, H], U32, align_bytes=64)
         w_scales = const.tile([P, E, H], U8, align_bytes=64)
+        identity = const.tile([P, P], F32)
+        same_batch = const.tile([P, GROUP], F32)
 
-        def softmax_over_agents(pool):
-            shape = [P, TILES, AGENTS, E]
-            raw = pool.tile(shape, BF16)
+        def load_logits(pool):
+            raw = pool.tile([P, TILES, AGENTS, E], BF16)
             nc.sync.dma_start(out=raw[:], in_=logits.rearrange("(t p) n e -> p t n e", p=P))
-            top = pool.tile([P, TILES, E], F32)
-            nc.vector.tensor_reduce(out=top[:], in_=raw[:].rearrange("p t n e -> p t e n"), axis=AX.X, op=ALU.max)
-            ex = pool.tile(shape, F32)
-            nc.vector.tensor_tensor(out=ex[:], in0=raw[:], in1=top[:].unsqueeze(2).to_broadcast(shape), op=ALU.subtract)
+            return raw
+
+        def softmax_over_agents(raw, tiles, pool, tag):
+            shape = [P, len(tiles), AGENTS, E]
+            logit = raw[:, tiles[0] : tiles[-1] + 1]
+            top = pool.tile([P, len(tiles), E], F32, tag="top" + tag)
+            nc.vector.tensor_reduce(out=top[:], in_=logit.rearrange("p t n e -> p t e n"), axis=AX.X, op=ALU.max)
+            ex = pool.tile(shape, F32, tag="ex" + tag)
+            nc.vector.tensor_tensor(out=ex[:], in0=logit, in1=top[:].unsqueeze(2).to_broadcast(shape), op=ALU.subtract)
             flat = ex[:].rearrange("p t n e -> p (t n e)")
             nc.scalar.activation(out=flat, in_=flat, func=ACT.Exp)
-            total = pool.tile([P, TILES, E], F32)
+            total = pool.tile([P, len(tiles), E], F32, tag="total" + tag)
             nc.vector.tensor_reduce(out=total[:], in_=ex[:].rearrange("p t n e -> p t e n"), axis=AX.X, op=ALU.add)
-            inverse = pool.tile([P, TILES, E], F32)
+            inverse = pool.tile([P, len(tiles), E], F32, tag="inverse" + tag)
             nc.vector.reciprocal(out=inverse[:], in_=total[:])
             nc.vector.tensor_tensor(
-                out=disp[:], in0=ex[:], in1=inverse[:].unsqueeze(2).to_broadcast(shape), op=ALU.mult
+                out=disp[:, tiles[0] : tiles[-1] + 1], in0=ex[:], in1=inverse[:].unsqueeze(2).to_broadcast(shape),
+                op=ALU.mult,
             )
 
-        def quantise_weights(e, pool):
+        def load_rows(half):
+            cols = slice(half * HALF * H, (half + 1) * HALF * H)
+            experts = slice(half * HALF, (half + 1) * HALF)
+            for rows, vector in ((bias_rows, b1), (gain_rows, g1), (shift_rows, be1)):
+                nc.sync.dma_start(
+                    out=rows[:, cols], in_=vector[experts].rearrange("e h -> (e h)").partition_broadcast(P)
+                )
+
+        weight_words = {}
+
+        def weights_words(e, pool):
             rows = pool.tile([P, PACK, H], BF16)
             nc.sync.dma_start(out=rows[:], in_=W1[e].rearrange("(p t) h -> p t h", t=PACK))
             words = pool.tile([P, H, PACK], BF16, align_bytes=64)
-            dst = words[:].rearrange("p (c i) t -> p c t i", i=4)
-            src = rows[:].rearrange("p t (c i) -> p c t i", i=4)
-            if e % 2 == 1:
-                nc.vector.tensor_copy(out=dst, in_=src)
-            else:
-                nc.scalar.copy(out=dst, in_=src)
+            nc.scalar.copy(
+                out=words[:].rearrange("p (c i) t -> p c t i", i=4), in_=rows[:].rearrange("p t (c i) -> p c t i", i=4)
+            )
+            weight_words[e] = words
+
+        def weights_codes(e):
             nc.vector.quantize_mx(
                 out=w_codes[:, e, :].bitcast(FP8X4),
                 scales=w_scales[:, e, :],
-                in_=words[:].rearrange("p h t -> p (h t)"),
+                in_=weight_words[e][:].rearrange("p h t -> p (h t)"),
             )
 
         product_tiles = [bt for bt in range(TILES) if bt not in BLOCK_TILES]
         made = {"product": 0, "block": 0}
-        current = {}
+        current = {"beat": 0}
         slot_codes = {}
+        ready = set()
+        summed, copied = [], []
+        grouped = []
+        block_done = {}
+        cast = []
 
-        def quantise_slots(bt, words):
-            codes = code_pool.tile([P, E * P], U32, align_bytes=64)
-            scales = code_pool.tile([P, E * P], U8, align_bytes=64)
-            nc.vector.quantize_mx(
-                out=codes[:].bitcast(FP8X4), scales=scales[:], in_=words[:].rearrange("p e b t -> p (e b t)")
-            )
+        def new_codes(bt):
+            codes = code_pool.tile([P, E, P], U32, align_bytes=64)
+            scales = code_pool.tile([P, E, P], U8, align_bytes=64)
             slot_codes[bt] = (codes, scales)
+
+        def load_tokens(bt):
+            tok = tok_pool.tile([P, AGENTS, K], BF16)
+            for pair in range(0, AGENTS, 2):
+                nc.sync.dma_start(out=tok[:, pair : pair + 2], in_=tokens[bt * P : (bt + 1) * P, pair : pair + 2])
+            current["tokens", bt] = tok
 
         def product_unit():
             unit = made["product"]
             if unit == E * len(product_tiles):
                 return
             made["product"] = unit + 1
-            bt, e = product_tiles[unit // E], unit % E
+            which, e = divmod(unit, E)
+            bt = product_tiles[which]
             if e == 0:
-                tok = tok_pool.tile([P, AGENTS, K], BF16)
-                nc.sync.dma_start(out=tok[:], in_=tokens[bt * P : (bt + 1) * P])
-                words = slot_pool.tile([P, E, P, PACK], BF16, align_bytes=64, tag="product_words")
-                current["product"] = (tok, words)
-            tok, words = current["product"]
-            parts, on_scalar = PARTS, ON_SCALAR
-            sums = sum_pool.tile([P, parts, K], F32, tag="sums")
-            length = AGENTS // parts
-            by_word = lambda row: row.rearrange("b (p t) -> b t p", t=PACK)
-            for r in range(length):
-                for q in range(parts):
-                    n = q * length + r
+                new_codes(bt)
+                if which + 1 < len(product_tiles):
+                    load_tokens(product_tiles[which + 1])
+            tok = current["tokens", bt]
+            products = []
+            for pair in range(AGENTS // 2):
+                both = sum_pool.tile([P, 2, K], F32, tag="sums")
+                for i in range(2):
+                    n = 2 * pair + i
                     weight = disp[:, bt, n, e : e + 1]
-                    target = sums[:, q, :].rearrange("b (t p) -> b t p", t=PACK)
-                    if r > 0:
-                        nc.vector.scalar_tensor_tensor(
-                            out=target, in0=by_word(tok[:, n, :]), scalar=weight, in1=target,
-                            op0=ALU.mult, op1=ALU.add,
-                        )
-                    elif q < on_scalar:
-                        nc.scalar.activation(out=target, in_=by_word(tok[:, n, :]), func=ACT.Copy, scale=weight)
+                    target = both[:, i, :].rearrange("b (t p) -> b t p", t=PACK)
+                    source = tok[:, n, :].rearrange("b (p t) -> b t p", t=PACK)
+                    if n == 0 and unit < 16:
+                        nc.scalar.activation(out=target, in_=source, func=ACT.Copy, scale=weight)
                     else:
-                        nc.vector.tensor_scalar(
-                            out=target, in0=by_word(tok[:, n, :]), scalar1=weight, scalar2=None, op0=ALU.mult
-                        )
+                        nc.vector.tensor_scalar(out=target, in0=source, scalar1=weight, scalar2=None, op0=ALU.mult)
+                    products.append(both[:, i, :])
             bank = slot_banks.tile([P, PACK, P], F32, tag="bank")
             for t in range(PACK):
-                for q in range(parts):
+                for n in range(AGENTS):
                     nc.tensor.matmul(
-                        bank[:, t, :], lhsT=sums[:, q, t * P : (t + 1) * P], rhs=identity[:],
-                        is_transpose=True, start=(q == 0), stop=(q == parts - 1),
+                        bank[:, t, :], lhsT=products[n][:, t * P : (t + 1) * P], rhs=identity[:],
+                        is_transpose=True, start=(n == 0), stop=(n == AGENTS - 1),
                     )
-            nc.scalar.copy(out=words[:, e], in_=bank[:].rearrange("p t b -> p b t"))
-            if e == E - 1:
-                quantise_slots(bt, words)
+            summed.append((current["beat"], bt, e, bank))
+
+        def copy_product(age):
+            while len(summed) > 0 and current["beat"] - summed[0][0] >= age:
+                beat, bt, e, bank = summed[0]
+                summed.remove(summed[0])
+                words = slot_pool.tile([P, P, PACK], BF16, align_bytes=64)
+                nc.scalar.copy(out=words[:], in_=bank[:].rearrange("p t b -> p b t"))
+                copied.append((current["beat"], bt, e, words))
+
+        def quantise_product(age):
+            while len(copied) > 0 and current["beat"] - copied[0][0] >= age:
+                beat, bt, e, words = copied[0]
+                copied.remove(copied[0])
+                codes, scales = slot_codes[bt]
+                nc.vector.quantize_mx(
+                    out=codes[:, e].bitcast(FP8X4), scales=scales[:, e], in_=words[:].rearrange("p b t -> p (b t)")
+                )
+                ready.add((bt, e))
+
+        def load_group(unit):
+            first = BLOCK_TILES[unit // GROUPS] * P + unit % GROUPS * GROUP
+            rows = group_pool.tile([P, K], BF16)
+            nc.sync.dma_start(out=rows[:], in_=tokens[first : first + GROUP].rearrange("b n k -> (b n) k"))
+            current["rows", unit] = rows
+
+        def spread_weights(bt):
+            shape = [P, E, GROUP, AGENTS]
+            spread = sum_pool.tile(shape, F32, tag="sums")
+            nc.vector.tensor_tensor(
+                out=spread[:],
+                in0=disp[:, bt].rearrange("p n e -> p e n").unsqueeze(2).to_broadcast(shape),
+                in1=same_batch[:].unsqueeze(1).unsqueeze(3).to_broadcast(shape),
+                op=ALU.mult,
+            )
+            banks = []
+            for half in range(2):
+                bank = slot_banks.tile([P, PACK, P], F32, tag="bank")
+                for i in range(PACK):
+                    nc.tensor.transpose(
+                        bank[:, i, :], spread[:, half * PACK + i].rearrange("p c n -> p (c n)"), identity[:]
+                    )
+                banks.append(bank)
+            current["spread", bt] = banks
+
+        def copy_weights(bt):
+            new_codes(bt)
+            diag = diag_pool.tile([P, GROUPS, E, GROUP], F32)
+            for half in range(2):
+                nc.scalar.copy(
+                    out=diag[:, :, half * PACK : (half + 1) * PACK, :],
+                    in_=current["spread", bt][half][:].rearrange("p e (g c) -> p g e c", c=GROUP),
+                )
+            words = block_pool.tile([P, E, P, PACK], BF16, align_bytes=64)
+            current["block", bt] = (diag, words)
 
         def block_unit():
             unit = made["block"]
@@ -155,165 +223,256 @@ def tile_softmoedynamics_pa_t_kernel(tc, tokens, logits, W1, b1, g1, be1, out):
                 return
             made["block"] = unit + 1
             bt, g = BLOCK_TILES[unit // GROUPS], unit % GROUPS
-            if g == 0:
-                shape = [P, E, GROUP, AGENTS]
-                spread = sum_pool.tile(shape, F32, tag="sums")
-                nc.vector.tensor_tensor(
-                    out=spread[:],
-                    in0=disp[:, bt].rearrange("p n e -> p e n").unsqueeze(2).to_broadcast(shape),
-                    in1=same_batch[:].unsqueeze(1).unsqueeze(3).to_broadcast(shape),
-                    op=ALU.mult,
-                )
-                diag = diag_pool.tile([P, GROUPS, E, GROUP], F32)
-                for half in range(2):
-                    bank = slot_banks.tile([P, PACK, P], F32, tag="bank")
-                    for i in range(PACK):
-                        nc.tensor.transpose(
-                            bank[:, i, :], spread[:, half * PACK + i].rearrange("p c n -> p (c n)"), identity[:]
-                        )
-                    nc.scalar.copy(
-                        out=diag[:, :, half * PACK : (half + 1) * PACK, :],
-                        in_=bank[:].rearrange("p e (g c) -> p g e c", c=GROUP),
-                    )
-                words = slot_pool.tile([P, E, P, PACK], BF16, align_bytes=64, tag="block_words")
-                current["block"] = (diag, words)
-            diag, words = current["block"]
-            tok = group_pool.tile([P, K], BF16)
-            first = bt * P + g * GROUP
-            nc.sync.dma_start(out=tok[:], in_=tokens[first : first + GROUP].rearrange("b n k -> (b n) k"))
+            diag, words = current["block", bt]
+            if unit + 2 < GROUPS * len(BLOCK_TILES):
+                load_group(unit + 2)
             tok32 = group_pool.tile([P, K], F32)
             nc.scalar.copy(
-                out=tok32[:].rearrange("r (t p) -> r t p", t=PACK), in_=tok[:].rearrange("r (p t) -> r t p", t=PACK)
+                out=tok32[:].rearrange("r (t p) -> r t p", t=PACK),
+                in_=current["rows", unit][:].rearrange("r (p t) -> r t p", t=PACK),
             )
+            cast.append((current["beat"], g, tok32, diag, words, bt))
+
+        def multiply_block(age):
+            if len(cast) == 0 or current["beat"] - cast[0][0] < age:
+                return
+            beat, g, tok32, diag, words, bt = cast[0]
+            cast.remove(cast[0])
             bank = slot_banks.tile([P, PACK, P], F32, tag="bank")
             for t in range(PACK):
                 nc.tensor.matmul(
                     bank[:, t, :], lhsT=tok32[:, t * P : (t + 1) * P], rhs=diag[:, g].rearrange("p e c -> p (e c)"),
                     start=True, stop=True,
                 )
-            nc.scalar.copy(
-                out=words[:, :, g * GROUP : (g + 1) * GROUP, :],
-                in_=bank[:].rearrange("p t (e c) -> p e c t", c=GROUP),
+            grouped.append((current["beat"], g, bank, words, bt))
+
+        def copy_block(age):
+            while len(grouped) > 0 and current["beat"] - grouped[0][0] >= age:
+                beat, g, bank, words, bt = grouped[0]
+                grouped.remove(grouped[0])
+                block_done[bt] = block_done.get(bt, 0) + 1
+                nc.scalar.copy(
+                    out=words[:, :, g * GROUP : (g + 1) * GROUP, :],
+                    in_=bank[:].rearrange("p t (e c) -> p e c t", c=GROUP),
+                )
+
+        def quantise_block(bt, half):
+            diag, words = current["block", bt]
+            codes, scales = slot_codes[bt]
+            assert block_done[bt] == GROUPS
+            for e in range(half * HALF, (half + 1) * HALF):
+                ready.add((bt, e))
+            experts = slice(half * HALF, (half + 1) * HALF)
+            nc.vector.quantize_mx(
+                out=codes[:, experts].rearrange("p e b -> p (e b)").bitcast(FP8X4),
+                scales=scales[:, experts].rearrange("p e b -> p (e b)"),
+                in_=words[:, experts].rearrange("p e b t -> p (e b t)"),
             )
-            if g == GROUPS - 1:
-                quantise_slots(bt, words)
 
         work = {}
+        group_ends = [sum(MISH_GROUPS[: g + 1]) for g in range(len(MISH_GROUPS))]
+        finished = []
 
-        def layer_and_centre(bt):
-            if bt == TILES:
-                return
+        def layer(chunk, i):
+            bt, e = chunk // 2, chunk % 2 * HALF + i
             codes, scales = slot_codes[bt]
-            x = x_pool.tile([P, E, H], F32)
-            v = v_pool.tile([P, E, H], F32)
-            total = small.tile([P, E], F32)
-            minus_mean = small.tile([P, E], F32)
-            squares = small.tile([P, E], F32)
-            for e in range(E):
-                bank = layer_banks.tile([P, H], F32)
-                nc.tensor.matmul_mx(
-                    out=bank[:],
-                    lhsT=codes[:, e * P : (e + 1) * P].bitcast(FP8X4),
-                    lhsT_scale=scales[:, e * P : (e + 1) * P],
-                    rhs=w_codes[:, e, :].bitcast(FP8X4),
-                    rhs_scale=w_scales[:, e, :],
-                    start=True,
-                    stop=True,
-                )
-                nc.vector.scalar_tensor_tensor(
-                    out=x[:, e, :], in0=bank[:], scalar=1.0, in1=bias_rows[:, e * H : (e + 1) * H],
-                    op0=ALU.mult, op1=ALU.add, accum_out=total[:, e : e + 1],
-                )
-            nc.vector.tensor_scalar(out=minus_mean[:], in0=total[:], scalar1=-1.0 / H, scalar2=None, op0=ALU.mult)
-            for e in range(E):
-                unused = small.tile([P, H], BF16)
-                nc.scalar.activation(
-                    out=unused[:], in_=x[:, e, :], func=ACT.Square, bias=minus_mean[:, e : e + 1], scale=1.0,
-                    accum_out=squares[:, e : e + 1],
-                )
-                nc.vector.scalar_tensor_tensor(
-                    out=v[:, e, :], in0=x[:, e, :], scalar=minus_mean[:, e : e + 1],
-                    in1=gain_rows[:, e * H : (e + 1) * H], op0=ALU.add, op1=ALU.mult,
-                )
-            work[bt] = {"v": v, "squares": squares}
+            assert (bt, e) in ready, (bt, e)
+            if i == 0:
+                v = v_pool.tile([P, HALF, H], F32)
+                total = small.tile([P, HALF], F32)
+                minus_mean = small.tile([P, HALF], F32)
+                squares = small.tile([P, HALF], F32)
+                work[chunk] = {"v": v, "total": total, "minus_mean": minus_mean, "squares": squares, "banks": []}
+            bank = layer_banks.tile([P, H], F32)
+            nc.tensor.matmul_mx(
+                out=bank[:],
+                lhsT=codes[:, e].bitcast(FP8X4),
+                lhsT_scale=scales[:, e],
+                rhs=w_codes[:, e, :].bitcast(FP8X4),
+                rhs_scale=w_scales[:, e, :],
+                start=True,
+                stop=True,
+            )
+            work[chunk]["banks"].append(bank)
 
-        def inverse_std(bt):
-            if bt == TILES:
-                return
-            variance = small.tile([P, E], F32)
-            inverse = small.tile([P, E], F32)
+        def add_bias(chunk, i):
+            v, total, bank = work[chunk]["v"], work[chunk]["total"], work[chunk]["banks"][i]
+            e = chunk % 2 * HALF + i
+            nc.vector.scalar_tensor_tensor(
+                out=v[:, i, :], in0=bank[:], scalar=1.0, in1=bias_rows[:, e * H : (e + 1) * H],
+                op0=ALU.mult, op1=ALU.add, accum_out=total[:, i : i + 1],
+            )
+
+        def mean(chunk):
             nc.vector.tensor_scalar(
-                out=variance[:], in0=work[bt]["squares"][:], scalar1=1.0 / H, scalar2=EPS, op0=ALU.mult, op1=ALU.add
+                out=work[chunk]["minus_mean"][:], in0=work[chunk]["total"][:], scalar1=-1.0 / H, scalar2=None,
+                op0=ALU.mult,
+            )
+
+        def square(chunk, i):
+            unused = small.tile([P, H], BF16)
+            nc.scalar.activation(
+                out=unused[:], in_=work[chunk]["v"][:, i, :], func=ACT.Square,
+                bias=work[chunk]["minus_mean"][:, i : i + 1], scale=1.0, accum_out=work[chunk]["squares"][:, i : i + 1],
+            )
+
+        def centre(chunk, i):
+            v, e = work[chunk]["v"], chunk % 2 * HALF + i
+            nc.vector.scalar_tensor_tensor(
+                out=v[:, i, :], in0=v[:, i, :], scalar=work[chunk]["minus_mean"][:, i : i + 1],
+                in1=gain_rows[:, e * H : (e + 1) * H], op0=ALU.add, op1=ALU.mult,
+            )
+
+        def inverse_std(chunk):
+            variance = small.tile([P, HALF], F32)
+            inverse = small.tile([P, HALF], F32)
+            nc.vector.tensor_scalar(
+                out=variance[:], in0=work[chunk]["squares"][:], scalar1=1.0 / H, scalar2=EPS, op0=ALU.mult, op1=ALU.add
             )
             nc.gpsimd.tensor_tensor(out=inverse[:], in0=variance[:], in1=minus_half[:], op=ALU.pow)
-            work[bt]["inverse"] = inverse
+            work[chunk]["inverse"] = inverse
 
-        def scale_and_shift(bt):
-            if bt == TILES:
-                return
-            v, inverse = work[bt]["v"], work[bt]["inverse"]
-            for e in range(E):
-                nc.vector.scalar_tensor_tensor(
-                    out=v[:, e, :], in0=v[:, e, :], scalar=inverse[:, e : e + 1],
-                    in1=shift_rows[:, e * H : (e + 1) * H], op0=ALU.mult, op1=ALU.add,
-                )
+        def scale_and_shift(chunk, i):
+            v, e = work[chunk]["v"], chunk % 2 * HALF + i
+            nc.vector.scalar_tensor_tensor(
+                out=v[:, i, :], in0=v[:, i, :], scalar=work[chunk]["inverse"][:, i : i + 1],
+                in1=shift_rows[:, e * H : (e + 1) * H], op0=ALU.mult, op1=ALU.add,
+            )
 
-        def mish_exp(bt, pool):
-            if bt < 0:
-                return
-            u = pool.tile([P, E * H], F32)
-            work[bt]["u"] = u
-            v = work[bt]["v"][:].rearrange("p e h -> p (e h)")
-            for cols in HALVES:
-                nc.scalar.activation(out=u[:, cols], in_=v[:, cols], func=ACT.Exp)
+        def flat_v(chunk):
+            return work[chunk]["v"][:].rearrange("p e h -> p (e h)")
 
-        def mish_log(bt):
-            if bt < 0:
-                return
-            u = work[bt]["u"]
-            for cols in HALVES:
-                nc.scalar.activation(out=u[:, cols], in_=u[:, cols], func=ACT.Ln, bias=1.0, scale=1.0)
+        def mish_exp(chunk, pool):
+            u = pool.tile([P, HALF * H], F32)
+            work[chunk]["u"] = u
+            nc.scalar.activation(out=u[:], in_=flat_v(chunk), func=ACT.Exp)
+            if chunk + 1 in group_ends:
+                one = small.tile([P, 1], F32)
+                nc.gpsimd.tensor_scalar(out=one[:], in0=u[:, 0:1], scalar1=0.0, scalar2=None, op0=ALU.is_ge)
+                current["one"] = one
 
-        def mish_tanh(bt):
-            if bt < 0:
-                return
-            u = work[bt]["u"]
-            for cols in HALVES:
-                nc.scalar.activation(out=u[:, cols], in_=u[:, cols], func=ACT.Tanh)
+        def mish_log(chunk, pool):
+            u = work[chunk]["u"]
+            nc.scalar.activation(out=u[:], in_=u[:], func=ACT.Ln, bias=current["one"][:], scale=1.0)
 
-        def multiply_and_store(bt):
-            if bt < 0:
-                return
-            u = work[bt]["u"]
-            v = work[bt]["v"][:].rearrange("p e h -> p (e h)")
-            rows = out[bt * P : (bt + 1) * P].rearrange("b e h -> b (e h)")
-            for cols in HALVES:
-                nc.vector.tensor_tensor(out=u[:, cols], in0=v[:, cols], in1=u[:, cols], op=ALU.mult)
-                nc.sync.dma_start(out=rows[:, cols], in_=u[:, cols])
+        def mish_tanh(chunk, pool):
+            u = work[chunk]["u"]
+            nc.scalar.activation(out=u[:], in_=u[:], func=ACT.Tanh)
+            finished.append(chunk)
+
+        def multiply_and_store(left):
+            while len(finished) > left:
+                chunk = finished[0]
+                finished.remove(chunk)
+                store(chunk)
+
+        def store(chunk):
+            u = work[chunk]["u"]
+            nc.vector.tensor_tensor(out=u[:], in0=flat_v(chunk), in1=u[:], op=ALU.mult)
+            bt, first = chunk // 2, chunk % 2 * HALF
+            rows = out[bt * P : (bt + 1) * P, first : first + HALF].rearrange("b e h -> b (e h)")
+            nc.sync.dma_start(out=rows, in_=u[:])
+
+        mish_queue = []
+
+        def queue_mish(chunk):
+            mish_queue.append((mish_exp, chunk))
+            if chunk + 1 in group_ends:
+                size = MISH_GROUPS[group_ends.index(chunk + 1)]
+                members = range(chunk + 1 - size, chunk + 1)
+                mish_queue.extend([(mish_log, c) for c in members])
+                mish_queue.extend([(mish_tanh, c) for c in members])
+
+        def run_mish(count, pool):
+            for i in range(min(count, len(mish_queue))):
+                stage, chunk = mish_queue[0]
+                mish_queue.remove(mish_queue[0])
+                stage(chunk, pool)
 
         with tc.tile_pool(name="early", bufs=1) as early, tc.tile_pool(name="staging", bufs=2) as staging:
-            softmax_over_agents(early)
+            raw = load_logits(early)
+            load_tokens(product_tiles[0])
+            softmax_over_agents(raw, range(1), early, "_first")
+            make_identity(nc, identity[:])
+            nc.vector.tensor_reduce(
+                out=same_batch[:], in_=identity[:].rearrange("p (g c) -> p c g", c=GROUP), axis=AX.X, op=ALU.add
+            )
+            load_group(0)
+            load_group(1)
             for e in range(E):
-                block_unit()
+                current["beat"] += 1
+                if e >= HALF:
+                    layer(0, e - HALF)
                 product_unit()
-                quantise_weights(e, staging)
-            for rows, vector in ((bias_rows, b1), (gain_rows, g1), (shift_rows, be1)):
-                nc.sync.dma_start(out=rows[:], in_=vector.rearrange("e h -> (e h)").partition_broadcast(P))
-        mish_pool = ctx.enter_context(tc.tile_pool(name="mish_pool", bufs=2))
-        for j in range(-1, TILES):
-            mish_exp(j, mish_pool)
-            layer_and_centre(j + 1)
-            product_unit()
-            inverse_std(j + 1)
-            block_unit()
-            mish_log(j)
-            product_unit()
-            block_unit()
-            scale_and_shift(j + 1)
-            mish_tanh(j)
-            product_unit()
-            block_unit()
-            multiply_and_store(j)
-            product_unit()
-            block_unit()
-            product_unit()
+                if e >= 3:
+                    weights_codes(e - 3)
+                quantise_product(1)
+                if e == 1:
+                    load_rows(0)
+                    softmax_over_agents(raw, range(1, TILES), early, "_rest")
+                if e == 5:
+                    load_rows(1)
+                if e >= HALF + 1:
+                    add_bias(0, e - HALF - 1)
+                weights_words(e, staging)
+                copy_product(1)
+            weights_codes(5)
+            add_bias(0, 3)
+            mean(0)
+            weights_codes(6)
+            copy_product(0)
+            quantise_product(0)
+            weights_codes(7)
+            for i in range(1):
+                layer(1, i)
+        mish_pool = ctx.enter_context(tc.tile_pool(name="mish_pool", bufs=5))
+        for chunk in range(1, CHUNKS + 1):
+            before = chunk - 1
+            for i in range(HALF):
+                current["beat"] += 1
+                following, j = divmod(chunk * HALF + i + 1, HALF)
+                multiply_block(1)
+                quantise_product(2)
+                if following < CHUNKS:
+                    if j == 0 and following // 2 in BLOCK_TILES:
+                        if following % 2 == 0:
+                            multiply_block(0)
+                            copy_block(0)
+                            quantise_block(following // 2, 0)
+                            quantise_block(following // 2, 1)
+                    layer(following, j)
+                if chunk < CHUNKS:
+                    add_bias(chunk, i)
+                    if i == HALF - 1:
+                        mean(chunk)
+                if i == 1:
+                    square(before, 2)
+                    square(before, 3)
+                if i in (1, 2):
+                    centre(before, 2 * i - 2)
+                    centre(before, 2 * i - 1)
+                if i == 2:
+                    inverse_std(before)
+                if i in PRODUCTS_AT.get(chunk, (0, 2)):
+                    product_unit()
+                multiply_and_store(1)
+                if i == 3:
+                    for j in range(HALF):
+                        scale_and_shift(before, j)
+                if i == 1 and before > 0:
+                    queue_mish(before - 1)
+                run_mish((1, 1, 1, 1)[i], mish_pool)
+                if i == (0 if chunk == 1 else 1) and chunk in {1: 2, 3: 4, 7: 6}:
+                    spread_weights({1: 2, 3: 4, 7: 6}[chunk])
+                if i == (1 if chunk == 1 else 2) and chunk in {1: 2, 3: 4, 7: 6}:
+                    copy_weights({1: 2, 3: 4, 7: 6}[chunk])
+                copy_block(1)
+                if i in BLOCKS_AT.get(chunk, (1, 3)) and chunk < 12:
+                    block_unit()
+                copy_product(1)
+                if i == 0:
+                    square(before, 0)
+                    square(before, 1)
+        queue_mish(CHUNKS - 1)
+        run_mish(len(mish_queue), mish_pool)
+        multiply_and_store(0)

@@ -21,12 +21,13 @@ GROUPS = P // GROUP
 EPS = 1e-5
 FLOPS = 2 * B * E * K * H + 2 * B * E * AGENTS * K
 
-BLOCK_TILES = (2, 4, 6)
+BLOCK_TILES = (1, 3, 5)
 HALF = E // 2
 CHUNKS = 2 * TILES
-MISH_GROUPS = (2, 4, 4, 4, 1, 1)
-PRODUCTS_AT = {1: (0, 1, 2, 3), 2: (0, 1, 2, 3)}
-BLOCKS_AT = {1: (1, 2, 3), 2: (0, 1, 2, 3)}
+MISH_GROUPS = (2, 2, 2, 2, 2, 2, 2, 2)
+PRODUCT_BEATS = [u - E for u in range(E)] + [1.6 * u for u in range(4 * E)]
+BLOCK_BEATS = [-5 + 0.6 * g for g in range(GROUPS)] + [3 + 1.75 * g for g in range(GROUPS)] + [19 + 1.75 * g for g in range(GROUPS)]
+FIRST_ON_SCALAR = 24
 
 
 def tile_softmoedynamics_pa_t_kernel(tc, tokens, logits, W1, b1, g1, be1, out):
@@ -40,15 +41,16 @@ def tile_softmoedynamics_pa_t_kernel(tc, tokens, logits, W1, b1, g1, be1, out):
         slot_pool = ctx.enter_context(tc.tile_pool(name="slot_pool", bufs=3))
         block_pool = ctx.enter_context(tc.tile_pool(name="block_pool", bufs=1))
         code_pool = ctx.enter_context(tc.tile_pool(name="code_pool", bufs=3))
-        v_pool = ctx.enter_context(tc.tile_pool(name="v_pool", bufs=7))
+        v_pool = ctx.enter_context(tc.tile_pool(name="v_pool", bufs=8))
         small = ctx.enter_context(tc.tile_pool(name="small", bufs=3))
         slot_banks = ctx.enter_context(tc.psum_pool(name="slot_banks", bufs=4))
         layer_banks = ctx.enter_context(tc.psum_pool(name="layer_banks", bufs=4))
 
-        minus_half = const.tile([P, HALF], F32)
-        nc.vector.memset(minus_half[:], -0.5)
-        warm = const.tile([P, HALF], F32)
-        nc.scalar.activation(out=warm[:], in_=minus_half[:], func=ACT.Exp)
+        eps = const.tile([P, 1], F32)
+        nc.vector.memset(eps[:], 0.0)
+        nc.vector.tensor_scalar(out=eps[:], in0=eps[:], scalar1=EPS, scalar2=None, op0=ALU.add)
+        warm = const.tile([P, 1], F32)
+        nc.scalar.activation(out=warm[:], in_=eps[:], func=ACT.Exp)
 
         bias_rows = const.tile([P, E * H], BF16)
         gain_rows = const.tile([P, E * H], BF16)
@@ -96,7 +98,8 @@ def tile_softmoedynamics_pa_t_kernel(tc, tokens, logits, W1, b1, g1, be1, out):
             rows = pool.tile([P, PACK, H], BF16)
             nc.sync.dma_start(out=rows[:], in_=W1[e].rearrange("(p t) h -> p t h", t=PACK))
             words = pool.tile([P, H, PACK], BF16, align_bytes=64)
-            nc.scalar.copy(
+            copy = nc.vector.tensor_copy if e % 2 == 1 else nc.scalar.copy
+            copy(
                 out=words[:].rearrange("p (c i) t -> p c t i", i=4), in_=rows[:].rearrange("p t (c i) -> p c t i", i=4)
             )
             weight_words[e] = words
@@ -149,7 +152,7 @@ def tile_softmoedynamics_pa_t_kernel(tc, tokens, logits, W1, b1, g1, be1, out):
                     weight = disp[:, bt, n, e : e + 1]
                     target = both[:, i, :].rearrange("b (t p) -> b t p", t=PACK)
                     source = tok[:, n, :].rearrange("b (p t) -> b t p", t=PACK)
-                    if n == 0 and unit < 16:
+                    if n == 0 and unit >= FIRST_ON_SCALAR:
                         nc.scalar.activation(out=target, in_=source, func=ACT.Copy, scale=weight)
                     else:
                         nc.vector.tensor_scalar(out=target, in0=source, scalar1=weight, scalar2=None, op0=ALU.mult)
@@ -234,10 +237,12 @@ def tile_softmoedynamics_pa_t_kernel(tc, tokens, logits, W1, b1, g1, be1, out):
             cast.append((current["beat"], g, tok32, diag, words, bt))
 
         def multiply_block(age):
-            if len(cast) == 0 or current["beat"] - cast[0][0] < age:
-                return
-            beat, g, tok32, diag, words, bt = cast[0]
-            cast.remove(cast[0])
+            while len(cast) > 0 and current["beat"] - cast[0][0] >= age:
+                group = cast[0]
+                cast.remove(group)
+                multiply_group(*group[1:])
+
+        def multiply_group(g, tok32, diag, words, bt):
             bank = slot_banks.tile([P, PACK, P], F32, tag="bank")
             for t in range(PACK):
                 nc.tensor.matmul(
@@ -271,6 +276,7 @@ def tile_softmoedynamics_pa_t_kernel(tc, tokens, logits, W1, b1, g1, be1, out):
 
         work = {}
         group_ends = [sum(MISH_GROUPS[: g + 1]) for g in range(len(MISH_GROUPS))]
+        statistics = {}
         finished = []
 
         def layer(chunk, i):
@@ -281,7 +287,12 @@ def tile_softmoedynamics_pa_t_kernel(tc, tokens, logits, W1, b1, g1, be1, out):
                 v = v_pool.tile([P, HALF, H], F32)
                 total = small.tile([P, HALF], F32)
                 minus_mean = small.tile([P, HALF], F32)
-                squares = small.tile([P, HALF], F32)
+                group = sum(1 for end in group_ends if end <= chunk)
+                place = chunk - (group_ends[group] - MISH_GROUPS[group])
+                if place == 0:
+                    stats = small.tile([P, MISH_GROUPS[group] * HALF], F32)
+                    statistics[group] = stats
+                squares = statistics[group][:, place * HALF : (place + 1) * HALF]
                 work[chunk] = {"v": v, "total": total, "minus_mean": minus_mean, "squares": squares, "banks": []}
             bank = layer_banks.tile([P, H], F32)
             nc.tensor.matmul_mx(
@@ -323,19 +334,21 @@ def tile_softmoedynamics_pa_t_kernel(tc, tokens, logits, W1, b1, g1, be1, out):
                 in1=gain_rows[:, e * H : (e + 1) * H], op0=ALU.add, op1=ALU.mult,
             )
 
-        def inverse_std(chunk):
-            variance = small.tile([P, HALF], F32)
-            inverse = small.tile([P, HALF], F32)
-            nc.vector.tensor_scalar(
-                out=variance[:], in0=work[chunk]["squares"][:], scalar1=1.0 / H, scalar2=EPS, op0=ALU.mult, op1=ALU.add
-            )
-            nc.gpsimd.tensor_tensor(out=inverse[:], in0=variance[:], in1=minus_half[:], op=ALU.pow)
-            work[chunk]["inverse"] = inverse
+        def members_of(group):
+            return range(group_ends[group] - MISH_GROUPS[group], group_ends[group])
+
+        def log_variance(group, pool):
+            stats = statistics[group]
+            nc.scalar.activation(out=stats[:], in_=stats[:], func=ACT.Ln, bias=eps[:], scale=1.0 / H)
+
+        def inverse_std(group, pool):
+            stats = statistics[group]
+            nc.scalar.activation(out=stats[:], in_=stats[:], func=ACT.Exp, scale=-0.5)
 
         def scale_and_shift(chunk, i):
             v, e = work[chunk]["v"], chunk % 2 * HALF + i
             nc.vector.scalar_tensor_tensor(
-                out=v[:, i, :], in0=v[:, i, :], scalar=work[chunk]["inverse"][:, i : i + 1],
+                out=v[:, i, :], in0=v[:, i, :], scalar=work[chunk]["squares"][:, i : i + 1],
                 in1=shift_rows[:, e * H : (e + 1) * H], op0=ALU.mult, op1=ALU.add,
             )
 
@@ -348,7 +361,7 @@ def tile_softmoedynamics_pa_t_kernel(tc, tokens, logits, W1, b1, g1, be1, out):
             nc.scalar.activation(out=u[:], in_=flat_v(chunk), func=ACT.Exp)
             if chunk + 1 in group_ends:
                 one = small.tile([P, 1], F32)
-                nc.gpsimd.tensor_scalar(out=one[:], in0=u[:, 0:1], scalar1=0.0, scalar2=None, op0=ALU.is_ge)
+                nc.vector.tensor_scalar(out=one[:], in0=u[:, 0:1], scalar1=0.0, scalar2=None, op0=ALU.is_ge)
                 current["one"] = one
 
         def mish_log(chunk, pool):
@@ -359,6 +372,13 @@ def tile_softmoedynamics_pa_t_kernel(tc, tokens, logits, W1, b1, g1, be1, out):
             u = work[chunk]["u"]
             nc.scalar.activation(out=u[:], in_=u[:], func=ACT.Tanh)
             finished.append(chunk)
+            group = group_ends.index([end for end in group_ends if end > chunk][0])
+            if group + 1 < len(MISH_GROUPS):
+                place, size = chunk - members_of(group)[0], MISH_GROUPS[group]
+                later = members_of(group + 1)
+                for c in later[place * len(later) // size : (place + 1) * len(later) // size]:
+                    for i in range(HALF):
+                        scale_and_shift(c, i)
 
         def multiply_and_store(left):
             while len(finished) > left:
@@ -375,19 +395,53 @@ def tile_softmoedynamics_pa_t_kernel(tc, tokens, logits, W1, b1, g1, be1, out):
 
         mish_queue = []
 
-        def queue_mish(chunk):
-            mish_queue.append((mish_exp, chunk))
-            if chunk + 1 in group_ends:
-                size = MISH_GROUPS[group_ends.index(chunk + 1)]
-                members = range(chunk + 1 - size, chunk + 1)
-                mish_queue.extend([(mish_log, c) for c in members])
-                mish_queue.extend([(mish_tanh, c) for c in members])
+        for group in range(len(MISH_GROUPS)):
+            mish_queue.append((log_variance, group))
+            mish_queue.append((inverse_std, group))
+            if group > 0:
+                mish_queue.extend([(mish_tanh, c) for c in members_of(group - 1)])
+            mish_queue.extend([(mish_exp, c) for c in members_of(group)])
+            mish_queue.extend([(mish_log, c) for c in members_of(group)])
+        mish_queue.extend([(mish_tanh, c) for c in members_of(len(MISH_GROUPS) - 1)])
 
-        def run_mish(count, pool):
-            for i in range(min(count, len(mish_queue))):
-                stage, chunk = mish_queue[0]
+        def run_mish(count, squared, pool):
+            while len(mish_queue) > 0 and count > 0:
+                stage, what = mish_queue[0]
+                if stage == log_variance and group_ends[what] > squared:
+                    return
                 mish_queue.remove(mish_queue[0])
-                stage(chunk, pool)
+                stage(what, pool)
+                if stage == inverse_std and what == 0:
+                    for c in members_of(0):
+                        for i in range(HALF):
+                            scale_and_shift(c, i)
+                if stage not in (log_variance, inverse_std):
+                    count -= 1
+
+        pinned = {mybir.EngineType.PE, mybir.EngineType.DVE, mybir.EngineType.Activation}
+        ctx.enter_context(tc.manual_schedule(engines=pinned))
+
+        def start_units(beat):
+            for bt in BLOCK_TILES:
+                first = BLOCK_BEATS[BLOCK_TILES.index(bt) * GROUPS]
+                if int(first) - 2 == beat:
+                    spread_weights(bt)
+                if int(first) - 1 == beat:
+                    copy_weights(bt)
+
+        def start_products(beat):
+            while made["product"] < len(PRODUCT_BEATS) and PRODUCT_BEATS[made["product"]] <= beat:
+                product_unit()
+
+        def start_blocks(beat):
+            while made["block"] < len(BLOCK_BEATS) and BLOCK_BEATS[made["block"]] <= beat:
+                block_unit()
+
+        def finish_blocks():
+            for bt in BLOCK_TILES:
+                if block_done.get(bt, 0) == GROUPS and (bt, 0) not in ready:
+                    quantise_block(bt, 0)
+                    quantise_block(bt, 1)
 
         with tc.tile_pool(name="early", bufs=1) as early, tc.tile_pool(name="staging", bufs=2) as staging:
             raw = load_logits(early)
@@ -400,79 +454,68 @@ def tile_softmoedynamics_pa_t_kernel(tc, tokens, logits, W1, b1, g1, be1, out):
             load_group(0)
             load_group(1)
             for e in range(E):
-                current["beat"] += 1
-                if e >= HALF:
-                    layer(0, e - HALF)
-                product_unit()
-                if e >= 3:
-                    weights_codes(e - 3)
-                quantise_product(1)
+                beat = e - E
+                current["beat"] = beat
+                multiply_block(1)
+                if e == HALF + 2:
+                    for i in range(HALF):
+                        layer(0, i)
+                start_products(beat)
                 if e == 1:
                     load_rows(0)
                     softmax_over_agents(raw, range(1, TILES), early, "_rest")
+                start_units(beat)
+                if e >= 2:
+                    weights_codes(e - 2)
+                quantise_product(1)
                 if e == 5:
                     load_rows(1)
-                if e >= HALF + 1:
-                    add_bias(0, e - HALF - 1)
+                if e >= HALF + 2:
+                    add_bias(0, 2 * e - 12)
+                    add_bias(0, 2 * e - 11)
                 weights_words(e, staging)
+                copy_block(1)
+                start_blocks(beat)
                 copy_product(1)
-            weights_codes(5)
-            add_bias(0, 3)
             mean(0)
             weights_codes(6)
             copy_product(0)
             quantise_product(0)
             weights_codes(7)
-            for i in range(1):
-                layer(1, i)
+            layer(1, 0)
+            layer(1, 1)
         mish_pool = ctx.enter_context(tc.tile_pool(name="mish_pool", bufs=5))
         for chunk in range(1, CHUNKS + 1):
             before = chunk - 1
             for i in range(HALF):
-                current["beat"] += 1
-                following, j = divmod(chunk * HALF + i + 1, HALF)
-                multiply_block(1)
+                beat = (chunk - 1) * HALF + i
+                current["beat"] = beat
                 quantise_product(2)
-                if following < CHUNKS:
-                    if j == 0 and following // 2 in BLOCK_TILES:
-                        if following % 2 == 0:
-                            multiply_block(0)
-                            copy_block(0)
-                            quantise_block(following // 2, 0)
-                            quantise_block(following // 2, 1)
+                finish_blocks()
+                following, j = divmod(chunk * HALF + i + 1, HALF)
+                if i % 2 == 1 and following < CHUNKS:
                     layer(following, j)
+                    layer(following, j + 1)
+                multiply_block(1)
+                start_products(beat)
+                if i == 0:
+                    square(before, 0)
+                    square(before, 1)
+                run_mish(1, chunk if i > 2 else before, mish_pool)
+                copy_block(1)
+                start_units(beat)
+                start_blocks(beat)
+                copy_product(2)
+                if i in (1, 2):
+                    centre(before, 2 * i - 2)
+                    centre(before, 2 * i - 1)
+                if i == 1:
+                    square(before, 2)
+                    square(before, 3)
                 if chunk < CHUNKS:
                     add_bias(chunk, i)
                     if i == HALF - 1:
                         mean(chunk)
-                if i == 1:
-                    square(before, 2)
-                    square(before, 3)
-                if i in (1, 2):
-                    centre(before, 2 * i - 2)
-                    centre(before, 2 * i - 1)
-                if i == 2:
-                    inverse_std(before)
-                if i in PRODUCTS_AT.get(chunk, (0, 2)):
-                    product_unit()
                 multiply_and_store(1)
-                if i == 3:
-                    for j in range(HALF):
-                        scale_and_shift(before, j)
-                if i == 1 and before > 0:
-                    queue_mish(before - 1)
-                run_mish((1, 1, 1, 1)[i], mish_pool)
-                if i == (0 if chunk == 1 else 1) and chunk in {1: 2, 3: 4, 7: 6}:
-                    spread_weights({1: 2, 3: 4, 7: 6}[chunk])
-                if i == (1 if chunk == 1 else 2) and chunk in {1: 2, 3: 4, 7: 6}:
-                    copy_weights({1: 2, 3: 4, 7: 6}[chunk])
-                copy_block(1)
-                if i in BLOCKS_AT.get(chunk, (1, 3)) and chunk < 12:
-                    block_unit()
-                copy_product(1)
-                if i == 0:
-                    square(before, 0)
-                    square(before, 1)
-        queue_mish(CHUNKS - 1)
-        run_mish(len(mish_queue), mish_pool)
+        run_mish(len(mish_queue), CHUNKS, mish_pool)
         multiply_and_store(0)

@@ -26,8 +26,9 @@ HALF = E // 2
 CHUNKS = 2 * TILES
 MISH_GROUPS = (2, 2, 2, 2, 2, 2, 2, 2)
 PRODUCT_BEATS = [u - E for u in range(E)] + [1.6 * u for u in range(4 * E)]
-BLOCK_BEATS = [-5 + 0.6 * g for g in range(GROUPS)] + [3 + 1.75 * g for g in range(GROUPS)] + [19 + 1.75 * g for g in range(GROUPS)]
-FIRST_ON_SCALAR = 24
+BLOCK_BEATS = [-6 + 0.75 * g for g in range(GROUPS)] + [3 + 1.75 * g for g in range(GROUPS)] + [19 + 1.75 * g for g in range(GROUPS)]
+FIRST_ON_SCALAR = 8
+PARTS_FIRST = 6
 
 
 def tile_softmoedynamics_pa_t_kernel(tc, tokens, logits, W1, b1, g1, be1, out):
@@ -145,7 +146,8 @@ def tile_softmoedynamics_pa_t_kernel(tc, tokens, logits, W1, b1, g1, be1, out):
                     load_tokens(product_tiles[which + 1])
             tok = current["tokens", bt]
             products = []
-            for pair in range(AGENTS // 2):
+            parts = PARTS_FIRST if unit < E else AGENTS
+            for pair in range(parts // 2):
                 both = sum_pool.tile([P, 2, K], F32, tag="sums")
                 for i in range(2):
                     n = 2 * pair + i
@@ -157,12 +159,18 @@ def tile_softmoedynamics_pa_t_kernel(tc, tokens, logits, W1, b1, g1, be1, out):
                     else:
                         nc.vector.tensor_scalar(out=target, in0=source, scalar1=weight, scalar2=None, op0=ALU.mult)
                     products.append(both[:, i, :])
+            for n in range(parts, AGENTS):
+                target = products[n - parts].rearrange("b (t p) -> b t p", t=PACK)
+                nc.vector.scalar_tensor_tensor(
+                    out=target, in0=tok[:, n, :].rearrange("b (p t) -> b t p", t=PACK),
+                    scalar=disp[:, bt, n, e : e + 1], in1=target, op0=ALU.mult, op1=ALU.add,
+                )
             bank = slot_banks.tile([P, PACK, P], F32, tag="bank")
             for t in range(PACK):
-                for n in range(AGENTS):
+                for n in range(parts):
                     nc.tensor.matmul(
                         bank[:, t, :], lhsT=products[n][:, t * P : (t + 1) * P], rhs=identity[:],
-                        is_transpose=True, start=(n == 0), stop=(n == AGENTS - 1),
+                        is_transpose=True, start=(n == 0), stop=(n == parts - 1),
                     )
             summed.append((current["beat"], bt, e, bank))
 
@@ -359,14 +367,10 @@ def tile_softmoedynamics_pa_t_kernel(tc, tokens, logits, W1, b1, g1, be1, out):
             u = pool.tile([P, HALF * H], F32)
             work[chunk]["u"] = u
             nc.scalar.activation(out=u[:], in_=flat_v(chunk), func=ACT.Exp)
-            if chunk + 1 in group_ends:
-                one = small.tile([P, 1], F32)
-                nc.vector.tensor_scalar(out=one[:], in0=u[:, 0:1], scalar1=0.0, scalar2=None, op0=ALU.is_ge)
-                current["one"] = one
 
         def mish_log(chunk, pool):
             u = work[chunk]["u"]
-            nc.scalar.activation(out=u[:], in_=u[:], func=ACT.Ln, bias=current["one"][:], scale=1.0)
+            nc.scalar.activation(out=u[:], in_=u[:], func=ACT.Ln, bias=1.0, scale=1.0)
 
         def mish_tanh(chunk, pool):
             u = work[chunk]["u"]
@@ -443,10 +447,10 @@ def tile_softmoedynamics_pa_t_kernel(tc, tokens, logits, W1, b1, g1, be1, out):
                     quantise_block(bt, 0)
                     quantise_block(bt, 1)
 
-        with tc.tile_pool(name="early", bufs=1) as early, tc.tile_pool(name="staging", bufs=2) as staging:
+        with tc.tile_pool(name="early", bufs=1) as early, tc.tile_pool(name="staging", bufs=4) as staging:
             raw = load_logits(early)
             load_tokens(product_tiles[0])
-            softmax_over_agents(raw, range(1), early, "_first")
+            softmax_over_agents(raw, range(2), early, "_first")
             make_identity(nc, identity[:])
             nc.vector.tensor_reduce(
                 out=same_batch[:], in_=identity[:].rearrange("p (g c) -> p c g", c=GROUP), axis=AX.X, op=ALU.add
@@ -457,31 +461,33 @@ def tile_softmoedynamics_pa_t_kernel(tc, tokens, logits, W1, b1, g1, be1, out):
                 beat = e - E
                 current["beat"] = beat
                 multiply_block(1)
-                if e == HALF + 2:
-                    for i in range(HALF):
-                        layer(0, i)
+                if e in (HALF + 2, HALF + 3):
+                    layer(0, 2 * (e - HALF - 2))
+                    layer(0, 2 * (e - HALF - 2) + 1)
                 start_products(beat)
                 if e == 1:
                     load_rows(0)
-                    softmax_over_agents(raw, range(1, TILES), early, "_rest")
+                    softmax_over_agents(raw, range(2, TILES), early, "_rest")
                 start_units(beat)
-                if e >= 2:
-                    weights_codes(e - 2)
+                if e >= 3:
+                    weights_codes(e - 3)
                 quantise_product(1)
                 if e == 5:
                     load_rows(1)
-                if e >= HALF + 2:
-                    add_bias(0, 2 * e - 12)
-                    add_bias(0, 2 * e - 11)
+                if e == HALF + 3:
+                    add_bias(0, 0)
+                    add_bias(0, 1)
                 weights_words(e, staging)
                 copy_block(1)
                 start_blocks(beat)
                 copy_product(1)
+            add_bias(0, 2)
+            add_bias(0, 3)
             mean(0)
-            weights_codes(6)
+            for e in range(E - 3, E):
+                weights_codes(e)
             copy_product(0)
             quantise_product(0)
-            weights_codes(7)
             layer(1, 0)
             layer(1, 1)
         mish_pool = ctx.enter_context(tc.tile_pool(name="mish_pool", bufs=5))

@@ -25,9 +25,11 @@ BLOCK_TILES = (1, 3, 5)
 HALF = E // 2
 CHUNKS = 2 * TILES
 MISH_GROUPS = (2, 2, 2, 2, 2, 2, 2, 2)
-PRODUCT_BEATS = [u - E for u in range(E)] + [1.6 * u for u in range(4 * E)]
-BLOCK_BEATS = [-6 + 0.75 * g for g in range(GROUPS)] + [3 + 1.75 * g for g in range(GROUPS)] + [19 + 1.75 * g for g in range(GROUPS)]
-FIRST_ON_SCALAR = 8
+PRODUCT_BEATS = [u - E for u in range(E)] + [1.7 * u for u in range(4 * E)]
+BLOCK_BEATS = (
+    [-6 + 0.75 * g for g in range(GROUPS)] + [2 + 1.75 * g for g in range(GROUPS)] + [18 + 1.75 * g for g in range(GROUPS)]
+)
+FIRST_ON_SCALAR = 2 * E
 PARTS_FIRST = 6
 
 
@@ -47,6 +49,8 @@ def tile_softmoedynamics_pa_t_kernel(tc, tokens, logits, W1, b1, g1, be1, out):
         slot_banks = ctx.enter_context(tc.psum_pool(name="slot_banks", bufs=4))
         layer_banks = ctx.enter_context(tc.psum_pool(name="layer_banks", bufs=4))
 
+        minus_half = const.tile([P, 2 * HALF], F32)
+        nc.vector.memset(minus_half[:], -0.5)
         eps = const.tile([P, 1], F32)
         nc.vector.memset(eps[:], 0.0)
         nc.vector.tensor_scalar(out=eps[:], in0=eps[:], scalar1=EPS, scalar2=None, op0=ALU.add)
@@ -353,7 +357,27 @@ def tile_softmoedynamics_pa_t_kernel(tc, tokens, logits, W1, b1, g1, be1, out):
             stats = statistics[group]
             nc.scalar.activation(out=stats[:], in_=stats[:], func=ACT.Exp, scale=-0.5)
 
+        to_scale = []
+
+        def power(group):
+            stats = statistics[group]
+            nc.vector.tensor_scalar(
+                out=stats[:], in0=stats[:], scalar1=1.0 / H, scalar2=EPS, op0=ALU.mult, op1=ALU.add
+            )
+            nc.gpsimd.tensor_tensor(
+                out=stats[:], in0=stats[:], in1=minus_half[:, : MISH_GROUPS[group] * HALF], op=ALU.pow
+            )
+            to_scale.extend([(c, i) for c in members_of(group) for i in range(HALF)])
+
+        def scale_some(count):
+            while len(to_scale) > 0 and count > 0:
+                c, i = to_scale[0]
+                to_scale.remove((c, i))
+                scale_and_shift(c, i)
+                count -= 1
+
         def scale_and_shift(chunk, i):
+            ready.add(("v", chunk, i))
             v, e = work[chunk]["v"], chunk % 2 * HALF + i
             nc.vector.scalar_tensor_tensor(
                 out=v[:, i, :], in0=v[:, i, :], scalar=work[chunk]["squares"][:, i : i + 1],
@@ -377,7 +401,7 @@ def tile_softmoedynamics_pa_t_kernel(tc, tokens, logits, W1, b1, g1, be1, out):
             nc.scalar.activation(out=u[:], in_=u[:], func=ACT.Tanh)
             finished.append(chunk)
             group = group_ends.index([end for end in group_ends if end > chunk][0])
-            if group + 1 < len(MISH_GROUPS):
+            if group + 1 < len(MISH_GROUPS) and group + 1 != 0:
                 place, size = chunk - members_of(group)[0], MISH_GROUPS[group]
                 later = members_of(group + 1)
                 for c in later[place * len(later) // size : (place + 1) * len(later) // size]:
@@ -400,8 +424,9 @@ def tile_softmoedynamics_pa_t_kernel(tc, tokens, logits, W1, b1, g1, be1, out):
         mish_queue = []
 
         for group in range(len(MISH_GROUPS)):
-            mish_queue.append((log_variance, group))
-            mish_queue.append((inverse_std, group))
+            if group != 0:
+                mish_queue.append((log_variance, group))
+                mish_queue.append((inverse_std, group))
             if group > 0:
                 mish_queue.extend([(mish_tanh, c) for c in members_of(group - 1)])
             mish_queue.extend([(mish_exp, c) for c in members_of(group)])
@@ -413,17 +438,30 @@ def tile_softmoedynamics_pa_t_kernel(tc, tokens, logits, W1, b1, g1, be1, out):
                 stage, what = mish_queue[0]
                 if stage == log_variance and group_ends[what] > squared:
                     return
+                if stage == mish_exp and ("v", what, HALF - 1) not in ready:
+                    return
                 mish_queue.remove(mish_queue[0])
                 stage(what, pool)
-                if stage == inverse_std and what == 0:
-                    for c in members_of(0):
-                        for i in range(HALF):
-                            scale_and_shift(c, i)
                 if stage not in (log_variance, inverse_std):
                     count -= 1
 
         pinned = {mybir.EngineType.PE, mybir.EngineType.DVE, mybir.EngineType.Activation}
         ctx.enter_context(tc.manual_schedule(engines=pinned))
+
+        def add_bias_and_mean(chunk, i):
+            if chunk < CHUNKS:
+                add_bias(chunk, i)
+                if i == HALF - 1:
+                    mean(chunk)
+
+        def layer_pair(chunk, first):
+            if chunk < CHUNKS:
+                layer(chunk, first)
+                layer(chunk, first + 1)
+
+        def quantise_slots(age):
+            quantise_product(age)
+            finish_blocks()
 
         def start_units(beat):
             for bt in BLOCK_TILES:
@@ -460,17 +498,20 @@ def tile_softmoedynamics_pa_t_kernel(tc, tokens, logits, W1, b1, g1, be1, out):
             for e in range(E):
                 beat = e - E
                 current["beat"] = beat
-                multiply_block(1)
-                if e in (HALF + 2, HALF + 3):
-                    layer(0, 2 * (e - HALF - 2))
-                    layer(0, 2 * (e - HALF - 2) + 1)
+                multiply_block(0)
+                if e == HALF + 2:
+                    layer(0, 0)
+                    layer(0, 1)
+                if e == HALF + 3:
+                    layer(0, 2)
+                    layer(0, 3)
                 start_products(beat)
                 if e == 1:
                     load_rows(0)
                     softmax_over_agents(raw, range(2, TILES), early, "_rest")
                 start_units(beat)
-                if e >= 3:
-                    weights_codes(e - 3)
+                if e >= 2:
+                    weights_codes(e - 2)
                 quantise_product(1)
                 if e == 5:
                     load_rows(1)
@@ -484,7 +525,7 @@ def tile_softmoedynamics_pa_t_kernel(tc, tokens, logits, W1, b1, g1, be1, out):
             add_bias(0, 2)
             add_bias(0, 3)
             mean(0)
-            for e in range(E - 3, E):
+            for e in range(E - 2, E):
                 weights_codes(e)
             copy_product(0)
             quantise_product(0)
@@ -496,32 +537,67 @@ def tile_softmoedynamics_pa_t_kernel(tc, tokens, logits, W1, b1, g1, be1, out):
             for i in range(HALF):
                 beat = (chunk - 1) * HALF + i
                 current["beat"] = beat
-                quantise_product(2)
-                finish_blocks()
-                following, j = divmod(chunk * HALF + i + 1, HALF)
-                if i % 2 == 1 and following < CHUNKS:
-                    layer(following, j)
-                    layer(following, j + 1)
-                multiply_block(1)
-                start_products(beat)
                 if i == 0:
                     square(before, 0)
                     square(before, 1)
-                run_mish(1, chunk if i > 2 else before, mish_pool)
-                copy_block(1)
-                start_units(beat)
-                start_blocks(beat)
-                copy_product(2)
-                if i in (1, 2):
-                    centre(before, 2 * i - 2)
-                    centre(before, 2 * i - 1)
-                if i == 1:
+                    multiply_block(0)
+                    multiply_and_store(1)
+                    start_products(beat)
+                    copy_block(1)
+                    add_bias_and_mean(chunk, i)
+                    quantise_slots(2)
+                    start_units(beat)
+                    start_blocks(beat)
+                    run_mish(1, before, mish_pool)
+                    copy_product(2)
+                    scale_some(2)
+                elif i == 1:
+                    run_mish(1, before, mish_pool)
                     square(before, 2)
                     square(before, 3)
-                if chunk < CHUNKS:
-                    add_bias(chunk, i)
-                    if i == HALF - 1:
-                        mean(chunk)
-                multiply_and_store(1)
+                    quantise_slots(2)
+                    scale_some(2)
+                    multiply_and_store(1)
+                    layer_pair(chunk, 2)
+                    multiply_block(0)
+                    start_products(beat)
+                    copy_block(1)
+                    add_bias_and_mean(chunk, i)
+                    centre(before, 0)
+                    centre(before, 1)
+                    start_units(beat)
+                    start_blocks(beat)
+                    copy_product(2)
+                elif i == 2:
+                    run_mish(1, before, mish_pool)
+                    multiply_block(0)
+                    if chunk == group_ends[0]:
+                        power(0)
+                    multiply_and_store(1)
+                    start_products(beat)
+                    copy_block(1)
+                    add_bias_and_mean(chunk, i)
+                    centre(before, 2)
+                    centre(before, 3)
+                    scale_some(2)
+                    quantise_slots(2)
+                    start_units(beat)
+                    start_blocks(beat)
+                    copy_product(2)
+                else:
+                    quantise_slots(2)
+                    scale_some(2)
+                    multiply_and_store(1)
+                    add_bias_and_mean(chunk, i)
+                    multiply_block(0)
+                    layer_pair(chunk + 1, 0)
+                    start_products(beat)
+                    start_units(beat)
+                    start_blocks(beat)
+                    run_mish(1, chunk, mish_pool)
+                    copy_block(1)
+                    copy_product(2)
+        scale_some(len(to_scale))
         run_mish(len(mish_queue), CHUNKS, mish_pool)
+        assert len(mish_queue) == 0
         multiply_and_store(0)

@@ -46,8 +46,8 @@ def tile_softmoedynamics_pa_t_kernel(tc, tokens, logits, W1, b1, g1, be1, out):
         code_pool = ctx.enter_context(tc.tile_pool(name="code_pool", bufs=3))
         v_pool = ctx.enter_context(tc.tile_pool(name="v_pool", bufs=8))
         small = ctx.enter_context(tc.tile_pool(name="small", bufs=3))
-        slot_banks = ctx.enter_context(tc.psum_pool(name="slot_banks", bufs=4))
-        layer_banks = ctx.enter_context(tc.psum_pool(name="layer_banks", bufs=4))
+        slot_banks = ctx.enter_context(tc.psum_pool(name="slot_banks", bufs=5))
+        layer_banks = ctx.enter_context(tc.psum_pool(name="layer_banks", bufs=3))
 
         minus_half = const.tile([P, 2 * HALF], F32)
         nc.vector.memset(minus_half[:], -0.5)
@@ -103,7 +103,7 @@ def tile_softmoedynamics_pa_t_kernel(tc, tokens, logits, W1, b1, g1, be1, out):
             rows = pool.tile([P, PACK, H], BF16)
             nc.sync.dma_start(out=rows[:], in_=W1[e].rearrange("(p t) h -> p t h", t=PACK))
             words = pool.tile([P, H, PACK], BF16, align_bytes=64)
-            copy = nc.vector.tensor_copy if e % 2 == 1 else nc.scalar.copy
+            copy = nc.vector.tensor_copy if e >= E - 3 else nc.scalar.copy
             copy(
                 out=words[:].rearrange("p (c i) t -> p c t i", i=4), in_=rows[:].rearrange("p t (c i) -> p c t i", i=4)
             )
@@ -301,10 +301,14 @@ def tile_softmoedynamics_pa_t_kernel(tc, tokens, logits, W1, b1, g1, be1, out):
                 minus_mean = small.tile([P, HALF], F32)
                 group = sum(1 for end in group_ends if end <= chunk)
                 place = chunk - (group_ends[group] - MISH_GROUPS[group])
-                if place == 0:
-                    stats = small.tile([P, MISH_GROUPS[group] * HALF], F32)
-                    statistics[group] = stats
-                squares = statistics[group][:, place * HALF : (place + 1) * HALF]
+                if group == len(MISH_GROUPS) - 1:
+                    own = small.tile([P, HALF], F32)
+                    squares = own[:]
+                else:
+                    if place == 0:
+                        stats = small.tile([P, MISH_GROUPS[group] * HALF], F32)
+                        statistics[group] = stats
+                    squares = statistics[group][:, place * HALF : (place + 1) * HALF]
                 work[chunk] = {"v": v, "total": total, "minus_mean": minus_mean, "squares": squares, "banks": []}
             bank = layer_banks.tile([P, H], F32)
             nc.tensor.matmul_mx(
@@ -359,15 +363,10 @@ def tile_softmoedynamics_pa_t_kernel(tc, tokens, logits, W1, b1, g1, be1, out):
 
         to_scale = []
 
-        def power(group):
-            stats = statistics[group]
-            nc.vector.tensor_scalar(
-                out=stats[:], in0=stats[:], scalar1=1.0 / H, scalar2=EPS, op0=ALU.mult, op1=ALU.add
-            )
-            nc.gpsimd.tensor_tensor(
-                out=stats[:], in0=stats[:], in1=minus_half[:, : MISH_GROUPS[group] * HALF], op=ALU.pow
-            )
-            to_scale.extend([(c, i) for c in members_of(group) for i in range(HALF)])
+        def power(stats, chunks):
+            nc.vector.tensor_scalar(out=stats, in0=stats, scalar1=1.0 / H, scalar2=EPS, op0=ALU.mult, op1=ALU.add)
+            nc.gpsimd.tensor_tensor(out=stats, in0=stats, in1=minus_half[:, : len(chunks) * HALF], op=ALU.pow)
+            to_scale.extend([(c, i) for c in chunks for i in range(HALF)])
 
         def scale_some(count):
             while len(to_scale) > 0 and count > 0:
@@ -401,7 +400,7 @@ def tile_softmoedynamics_pa_t_kernel(tc, tokens, logits, W1, b1, g1, be1, out):
             nc.scalar.activation(out=u[:], in_=u[:], func=ACT.Tanh)
             finished.append(chunk)
             group = group_ends.index([end for end in group_ends if end > chunk][0])
-            if group + 1 < len(MISH_GROUPS) and group + 1 != 0:
+            if group + 1 < len(MISH_GROUPS) - 1:
                 place, size = chunk - members_of(group)[0], MISH_GROUPS[group]
                 later = members_of(group + 1)
                 for c in later[place * len(later) // size : (place + 1) * len(later) // size]:
@@ -421,10 +420,22 @@ def tile_softmoedynamics_pa_t_kernel(tc, tokens, logits, W1, b1, g1, be1, out):
             rows = out[bt * P : (bt + 1) * P, first : first + HALF].rearrange("b e h -> b (e h)")
             nc.sync.dma_start(out=rows, in_=u[:])
 
+        def finish_in_pieces(chunk):
+            u, v = work[chunk]["u"], work[chunk]["v"]
+            bt, first = chunk // 2, chunk % 2 * HALF
+            for i in range(HALF):
+                nc.scalar.activation(out=u[:, i * H : (i + 1) * H], in_=u[:, i * H : (i + 1) * H], func=ACT.Tanh)
+                nc.vector.tensor_tensor(
+                    out=u[:, i * H : (i + 1) * H], in0=v[:, i, :], in1=u[:, i * H : (i + 1) * H], op=ALU.mult
+                )
+                nc.sync.dma_start(
+                    out=out[bt * P : (bt + 1) * P, first + i], in_=u[:, i * H : (i + 1) * H]
+                )
+
         mish_queue = []
 
         for group in range(len(MISH_GROUPS)):
-            if group != 0:
+            if 0 < group < len(MISH_GROUPS) - 1:
                 mish_queue.append((log_variance, group))
                 mish_queue.append((inverse_std, group))
             if group > 0:
@@ -532,7 +543,7 @@ def tile_softmoedynamics_pa_t_kernel(tc, tokens, logits, W1, b1, g1, be1, out):
             layer(1, 0)
             layer(1, 1)
         mish_pool = ctx.enter_context(tc.tile_pool(name="mish_pool", bufs=5))
-        for chunk in range(1, CHUNKS + 1):
+        for chunk in range(1, CHUNKS - 1):
             before = chunk - 1
             for i in range(HALF):
                 beat = (chunk - 1) * HALF + i
@@ -572,7 +583,7 @@ def tile_softmoedynamics_pa_t_kernel(tc, tokens, logits, W1, b1, g1, be1, out):
                     run_mish(1, before, mish_pool)
                     multiply_block(0)
                     if chunk == group_ends[0]:
-                        power(0)
+                        power(statistics[0][:], members_of(0))
                     multiply_and_store(1)
                     start_products(beat)
                     copy_block(1)
@@ -597,7 +608,46 @@ def tile_softmoedynamics_pa_t_kernel(tc, tokens, logits, W1, b1, g1, be1, out):
                     run_mish(1, chunk, mish_pool)
                     copy_block(1)
                     copy_product(2)
-        scale_some(len(to_scale))
-        run_mish(len(mish_queue), CHUNKS, mish_pool)
-        assert len(mish_queue) == 0
+        last, before = CHUNKS - 1, CHUNKS - 2
+
+        def take(stage, chunk):
+            while (stage, chunk) in mish_queue:
+                run_mish(1, CHUNKS, mish_pool)
+
+        def squares_of(chunk):
+            for i in range(HALF):
+                square(chunk, i)
+
+        def norm(chunk):
+            for i in range(HALF):
+                centre(chunk, i)
+            power(work[chunk]["squares"], [chunk])
+
+        current["beat"] = CHUNKS * HALF
+        take(mish_tanh, last - 5)
+        copy_product(0)
+        quantise_slots(0)
+        layer_pair(last, 2)
+        add_bias(last, 0)
+        add_bias(last, 1)
+        squares_of(before)
         multiply_and_store(0)
+        add_bias(last, 2)
+        add_bias(last, 3)
+        mean(last)
+        take(mish_tanh, last - 4)
+        take(mish_exp, last - 3)
+        squares_of(last)
+        norm(before)
+        multiply_and_store(0)
+        take(mish_exp, last - 2)
+        norm(last)
+        take(mish_log, last - 2)
+        scale_some(2 * HALF)
+        take(mish_tanh, last - 3)
+        multiply_and_store(0)
+        take(mish_tanh, last - 2)
+        take(mish_log, last)
+        multiply_and_store(0)
+        for chunk in (before, last):
+            finish_in_pieces(chunk)

@@ -29,7 +29,8 @@ PRODUCT_BEATS = [u - E for u in range(E)] + [1.7 * u for u in range(4 * E)]
 BLOCK_BEATS = (
     [-6 + 0.75 * g for g in range(GROUPS)] + [2 + 1.75 * g for g in range(GROUPS)] + [18 + 1.75 * g for g in range(GROUPS)]
 )
-FIRST_ON_SCALAR = 2 * E
+AHEAD_UNITS = 2 * E
+TWO_ON_SCALAR = 4 * E
 PARTS_FIRST = 6
 
 
@@ -38,13 +39,15 @@ def tile_softmoedynamics_pa_t_kernel(tc, tokens, logits, W1, b1, g1, be1, out):
     with ExitStack() as ctx:
         const = ctx.enter_context(tc.tile_pool(name="const", bufs=1))
         tok_pool = ctx.enter_context(tc.tile_pool(name="tok_pool", bufs=2))
-        group_pool = ctx.enter_context(tc.tile_pool(name="group_pool", bufs=3))
+        rows_pool = ctx.enter_context(tc.tile_pool(name="rows_pool", bufs=3))
+        group_pool = ctx.enter_context(tc.tile_pool(name="group_pool", bufs=2))
+        unused_pool = ctx.enter_context(tc.tile_pool(name="unused_pool", bufs=2))
         diag_pool = ctx.enter_context(tc.tile_pool(name="diag_pool", bufs=1))
-        sum_pool = ctx.enter_context(tc.tile_pool(name="sum_pool", bufs=7))
+        sum_pool = ctx.enter_context(tc.tile_pool(name="sum_pool", bufs=8))
         slot_pool = ctx.enter_context(tc.tile_pool(name="slot_pool", bufs=3))
         block_pool = ctx.enter_context(tc.tile_pool(name="block_pool", bufs=1))
         code_pool = ctx.enter_context(tc.tile_pool(name="code_pool", bufs=3))
-        v_pool = ctx.enter_context(tc.tile_pool(name="v_pool", bufs=8))
+        v_pool = ctx.enter_context(tc.tile_pool(name="v_pool", bufs=7))
         small = ctx.enter_context(tc.tile_pool(name="small", bufs=3))
         slot_banks = ctx.enter_context(tc.psum_pool(name="slot_banks", bufs=5))
         layer_banks = ctx.enter_context(tc.psum_pool(name="layer_banks", bufs=3))
@@ -103,7 +106,7 @@ def tile_softmoedynamics_pa_t_kernel(tc, tokens, logits, W1, b1, g1, be1, out):
             rows = pool.tile([P, PACK, H], BF16)
             nc.sync.dma_start(out=rows[:], in_=W1[e].rearrange("(p t) h -> p t h", t=PACK))
             words = pool.tile([P, H, PACK], BF16, align_bytes=64)
-            copy = nc.vector.tensor_copy if e >= E - 3 else nc.scalar.copy
+            copy = nc.vector.tensor_copy if e % 2 == 1 else nc.scalar.copy
             copy(
                 out=words[:].rearrange("p (c i) t -> p c t i", i=4), in_=rows[:].rearrange("p t (c i) -> p c t i", i=4)
             )
@@ -137,6 +140,17 @@ def tile_softmoedynamics_pa_t_kernel(tc, tokens, logits, W1, b1, g1, be1, out):
                 nc.sync.dma_start(out=tok[:, pair : pair + 2], in_=tokens[bt * P : (bt + 1) * P, pair : pair + 2])
             current["tokens", bt] = tok
 
+        made_ahead = {}
+
+        def product(bt, e, n, both, on_scalar):
+            target = both[:, n % 2, :].rearrange("b (t p) -> b t p", t=PACK)
+            source = current["tokens", bt][:, n, :].rearrange("b (p t) -> b t p", t=PACK)
+            weight = disp[:, bt, n, e : e + 1]
+            if on_scalar:
+                nc.scalar.activation(out=target, in_=source, func=ACT.Copy, scale=weight)
+            else:
+                nc.vector.tensor_scalar(out=target, in0=source, scalar1=weight, scalar2=None, op0=ALU.mult)
+
         def product_unit():
             unit = made["product"]
             if unit == E * len(product_tiles):
@@ -148,27 +162,28 @@ def tile_softmoedynamics_pa_t_kernel(tc, tokens, logits, W1, b1, g1, be1, out):
                 new_codes(bt)
                 if which + 1 < len(product_tiles):
                     load_tokens(product_tiles[which + 1])
-            tok = current["tokens", bt]
             products = []
             parts = PARTS_FIRST if unit < E else AGENTS
-            for pair in range(parts // 2):
-                both = sum_pool.tile([P, 2, K], F32, tag="sums")
-                for i in range(2):
-                    n = 2 * pair + i
-                    weight = disp[:, bt, n, e : e + 1]
-                    target = both[:, i, :].rearrange("b (t p) -> b t p", t=PACK)
-                    source = tok[:, n, :].rearrange("b (p t) -> b t p", t=PACK)
-                    if n == 0 and unit >= FIRST_ON_SCALAR:
-                        nc.scalar.activation(out=target, in_=source, func=ACT.Copy, scale=weight)
+            for n in range(parts):
+                if n % 2 == 0:
+                    if n == 0 and unit in made_ahead:
+                        both = made_ahead[unit]
                     else:
-                        nc.vector.tensor_scalar(out=target, in0=source, scalar1=weight, scalar2=None, op0=ALU.mult)
-                    products.append(both[:, i, :])
+                        both = sum_pool.tile([P, 2, K], F32, tag="sums")
+                if not (n == 0 and unit in made_ahead):
+                    on_scalar = n == 0 and unit >= AHEAD_UNITS or n == AGENTS - 1 and unit >= TWO_ON_SCALAR
+                    product(bt, e, n, both, on_scalar)
+                products.append(both[:, n % 2, :])
             for n in range(parts, AGENTS):
-                target = products[n - parts].rearrange("b (t p) -> b t p", t=PACK)
+                target = products[1 + n - parts].rearrange("b (t p) -> b t p", t=PACK)
                 nc.vector.scalar_tensor_tensor(
-                    out=target, in0=tok[:, n, :].rearrange("b (p t) -> b t p", t=PACK),
+                    out=target, in0=current["tokens", bt][:, n, :].rearrange("b (p t) -> b t p", t=PACK),
                     scalar=disp[:, bt, n, e : e + 1], in1=target, op0=ALU.mult, op1=ALU.add,
                 )
+            if unit + 1 < AHEAD_UNITS and e + 1 < E:
+                both = sum_pool.tile([P, 2, K], F32, tag="sums")
+                product(bt, e + 1, 0, both, True)
+                made_ahead[unit + 1] = both
             bank = slot_banks.tile([P, PACK, P], F32, tag="bank")
             for t in range(PACK):
                 for n in range(parts):
@@ -198,7 +213,7 @@ def tile_softmoedynamics_pa_t_kernel(tc, tokens, logits, W1, b1, g1, be1, out):
 
         def load_group(unit):
             first = BLOCK_TILES[unit // GROUPS] * P + unit % GROUPS * GROUP
-            rows = group_pool.tile([P, K], BF16)
+            rows = rows_pool.tile([P, K], BF16)
             nc.sync.dma_start(out=rows[:], in_=tokens[first : first + GROUP].rearrange("b n k -> (b n) k"))
             current["rows", unit] = rows
 
@@ -337,10 +352,21 @@ def tile_softmoedynamics_pa_t_kernel(tc, tokens, logits, W1, b1, g1, be1, out):
             )
 
         def square(chunk, i):
-            unused = small.tile([P, H], BF16)
+            unused = unused_pool.tile([P, H], BF16)
             nc.scalar.activation(
                 out=unused[:], in_=work[chunk]["v"][:, i, :], func=ACT.Square,
                 bias=work[chunk]["minus_mean"][:, i : i + 1], scale=1.0, accum_out=work[chunk]["squares"][:, i : i + 1],
+            )
+
+        def square_on_vector(chunk, i):
+            both = sum_pool.tile([P, 2, K], F32, tag="sums")
+            nc.vector.tensor_scalar(
+                out=both[:, 0, :], in0=work[chunk]["v"][:, i, :], scalar1=work[chunk]["minus_mean"][:, i : i + 1],
+                scalar2=None, op0=ALU.add,
+            )
+            nc.vector.scalar_tensor_tensor(
+                out=both[:, 1, :], in0=both[:, 0, :], scalar=1.0, in1=both[:, 0, :],
+                op0=ALU.mult, op1=ALU.mult, accum_out=work[chunk]["squares"][:, i : i + 1],
             )
 
         def centre(chunk, i):
@@ -542,7 +568,7 @@ def tile_softmoedynamics_pa_t_kernel(tc, tokens, logits, W1, b1, g1, be1, out):
             quantise_product(0)
             layer(1, 0)
             layer(1, 1)
-        mish_pool = ctx.enter_context(tc.tile_pool(name="mish_pool", bufs=5))
+        mish_pool = ctx.enter_context(tc.tile_pool(name="mish_pool", bufs=6))
         for chunk in range(1, CHUNKS - 1):
             before = chunk - 1
             for i in range(HALF):
@@ -630,20 +656,24 @@ def tile_softmoedynamics_pa_t_kernel(tc, tokens, logits, W1, b1, g1, be1, out):
         layer_pair(last, 2)
         add_bias(last, 0)
         add_bias(last, 1)
+        take(mish_tanh, last - 4)
         squares_of(before)
-        multiply_and_store(0)
         add_bias(last, 2)
         add_bias(last, 3)
         mean(last)
-        take(mish_tanh, last - 4)
         take(mish_exp, last - 3)
-        squares_of(last)
+        square(last, 0)
+        square(last, 1)
         norm(before)
-        multiply_and_store(0)
         take(mish_exp, last - 2)
+        square_on_vector(last, 2)
+        square_on_vector(last, 3)
+        scale_some(HALF)
         norm(last)
+        multiply_and_store(1)
         take(mish_log, last - 2)
-        scale_some(2 * HALF)
+        scale_some(HALF)
+        multiply_and_store(0)
         take(mish_tanh, last - 3)
         multiply_and_store(0)
         take(mish_tanh, last - 2)

@@ -186,10 +186,11 @@ def tile_softmoedynamics_pa_t_kernel(tc, tokens, logits, W1, b1, g1, be1, out):
                 made_ahead[unit + 1] = both
             bank = slot_banks.tile([P, PACK, P], F32, tag="bank")
             for t in range(PACK):
-                for n in range(parts):
+                for place in range(parts):
+                    n = min(place // 4 * 4 + 3, parts - 1) - place % 4
                     nc.tensor.matmul(
                         bank[:, t, :], lhsT=products[n][:, t * P : (t + 1) * P], rhs=identity[:],
-                        is_transpose=True, start=(n == 0), stop=(n == parts - 1),
+                        is_transpose=True, start=(place == 0), stop=(place == parts - 1),
                     )
             summed.append((current["beat"], bt, e, bank))
 

@@ -106,7 +106,7 @@ def tile_softmoedynamics_pa_t_kernel(tc, tokens, logits, W1, b1, g1, be1, out):
             rows = pool.tile([P, PACK, H], BF16)
             nc.sync.dma_start(out=rows[:], in_=W1[e].rearrange("(p t) h -> p t h", t=PACK))
             words = pool.tile([P, H, PACK], BF16, align_bytes=64)
-            copy = nc.vector.tensor_copy if e % 2 == 1 else nc.scalar.copy
+            copy = nc.vector.tensor_copy if e in (2, 5) else nc.scalar.copy
             copy(
                 out=words[:].rearrange("p (c i) t -> p c t i", i=4), in_=rows[:].rearrange("p t (c i) -> p c t i", i=4)
             )
@@ -175,7 +175,7 @@ def tile_softmoedynamics_pa_t_kernel(tc, tokens, logits, W1, b1, g1, be1, out):
                     product(bt, e, n, both, on_scalar)
                 products.append(both[:, n % 2, :])
             for n in range(parts, AGENTS):
-                target = products[1 + n - parts].rearrange("b (t p) -> b t p", t=PACK)
+                target = products[n - 2].rearrange("b (t p) -> b t p", t=PACK)
                 nc.vector.scalar_tensor_tensor(
                     out=target, in0=current["tokens", bt][:, n, :].rearrange("b (p t) -> b t p", t=PACK),
                     scalar=disp[:, bt, n, e : e + 1], in1=target, op0=ALU.mult, op1=ALU.add,
@@ -587,7 +587,7 @@ def tile_softmoedynamics_pa_t_kernel(tc, tokens, logits, W1, b1, g1, be1, out):
                     start_units(beat)
                     start_blocks(beat)
                     run_mish(1, before, mish_pool)
-                    copy_product(2)
+                    copy_product(3)
                     scale_some(2)
                 elif i == 1:
                     run_mish(1, before, mish_pool)
@@ -605,7 +605,7 @@ def tile_softmoedynamics_pa_t_kernel(tc, tokens, logits, W1, b1, g1, be1, out):
                     centre(before, 1)
                     start_units(beat)
                     start_blocks(beat)
-                    copy_product(2)
+                    copy_product(3)
                 elif i == 2:
                     run_mish(1, before, mish_pool)
                     multiply_block(0)
@@ -621,7 +621,7 @@ def tile_softmoedynamics_pa_t_kernel(tc, tokens, logits, W1, b1, g1, be1, out):
                     quantise_slots(2)
                     start_units(beat)
                     start_blocks(beat)
-                    copy_product(2)
+                    copy_product(3)
                 else:
                     quantise_slots(2)
                     scale_some(2)
@@ -634,7 +634,7 @@ def tile_softmoedynamics_pa_t_kernel(tc, tokens, logits, W1, b1, g1, be1, out):
                     start_blocks(beat)
                     run_mish(1, chunk, mish_pool)
                     copy_block(1)
-                    copy_product(2)
+                    copy_product(3)
         last, before = CHUNKS - 1, CHUNKS - 2
 
         def take(stage, chunk):

@@ -42,8 +42,9 @@ def tile_softmoedynamics_pa_t_kernel(tc, tokens, logits, W1, b1, g1, be1, out):
         rows_pool = ctx.enter_context(tc.tile_pool(name="rows_pool", bufs=3))
         group_pool = ctx.enter_context(tc.tile_pool(name="group_pool", bufs=2))
         unused_pool = ctx.enter_context(tc.tile_pool(name="unused_pool", bufs=2))
-        diag_pool = ctx.enter_context(tc.tile_pool(name="diag_pool", bufs=1))
+        diag_pool = ctx.enter_context(tc.tile_pool(name="diag_pool", bufs=2))
         sum_pool = ctx.enter_context(tc.tile_pool(name="sum_pool", bufs=8))
+        gpsimd_pool = ctx.enter_context(tc.tile_pool(name="gpsimd_pool", bufs=2))
         slot_pool = ctx.enter_context(tc.tile_pool(name="slot_pool", bufs=3))
         block_pool = ctx.enter_context(tc.tile_pool(name="block_pool", bufs=1))
         code_pool = ctx.enter_context(tc.tile_pool(name="code_pool", bufs=3))
@@ -151,6 +152,26 @@ def tile_softmoedynamics_pa_t_kernel(tc, tokens, logits, W1, b1, g1, be1, out):
             else:
                 nc.vector.tensor_scalar(out=target, in0=source, scalar1=weight, scalar2=None, op0=ALU.mult)
 
+        handed = {}
+
+        def hand_over(beat):
+            unit = made["product"]
+            if unit < E or unit == E * len(product_tiles) or PRODUCT_BEATS[unit] > beat + 2:
+                return
+            bt, e = product_tiles[unit // E], unit % E
+            if ("tokens", bt) not in current:
+                return
+            n = 5
+            factor = small.tile([P, 1], F32)
+            nc.vector.tensor_copy(out=factor[:], in_=disp[:, bt, n, e : e + 1])
+            row = gpsimd_pool.tile([P, K], F32)
+            nc.gpsimd.tensor_scalar(
+                out=row[:].rearrange("b (t p) -> b t p", t=PACK),
+                in0=current["tokens", bt][:, n, :].rearrange("b (p t) -> b t p", t=PACK),
+                scalar1=factor[:], scalar2=0.0, op0=ALU.mult, op1=ALU.add,
+            )
+            handed[unit, n] = row[:]
+
         def product_unit():
             unit = made["product"]
             if unit == E * len(product_tiles):
@@ -163,15 +184,18 @@ def tile_softmoedynamics_pa_t_kernel(tc, tokens, logits, W1, b1, g1, be1, out):
                 if which + 1 < len(product_tiles):
                     load_tokens(product_tiles[which + 1])
             products = []
-            parts = PARTS_FIRST if unit < E else AGENTS
+            parts = (PARTS_FIRST if unit < E else AGENTS)
             for n in range(parts):
                 if n % 2 == 0:
                     if n == 0 and unit in made_ahead:
                         both = made_ahead[unit]
                     else:
                         both = sum_pool.tile([P, 2, K], F32, tag="sums")
+                if (unit, n) in handed:
+                    products.append(handed[unit, n])
+                    continue
                 if not (n == 0 and unit in made_ahead):
-                    on_scalar = n == 0 and unit >= AHEAD_UNITS or n == AGENTS - 1 and unit >= TWO_ON_SCALAR
+                    on_scalar = n == 0 and unit >= AHEAD_UNITS or n == AGENTS - 2 and unit >= TWO_ON_SCALAR
                     product(bt, e, n, both, on_scalar)
                 products.append(both[:, n % 2, :])
             for n in range(parts, AGENTS):
@@ -569,7 +593,7 @@ def tile_softmoedynamics_pa_t_kernel(tc, tokens, logits, W1, b1, g1, be1, out):
             quantise_product(0)
             layer(1, 0)
             layer(1, 1)
-        mish_pool = ctx.enter_context(tc.tile_pool(name="mish_pool", bufs=6))
+        mish_pool = ctx.enter_context(tc.tile_pool(name="mish_pool", bufs=5))
         for chunk in range(1, CHUNKS - 1):
             before = chunk - 1
             for i in range(HALF):
@@ -582,7 +606,6 @@ def tile_softmoedynamics_pa_t_kernel(tc, tokens, logits, W1, b1, g1, be1, out):
                     multiply_and_store(1)
                     start_products(beat)
                     copy_block(1)
-                    add_bias_and_mean(chunk, i)
                     quantise_slots(2)
                     start_units(beat)
                     start_blocks(beat)
@@ -593,6 +616,9 @@ def tile_softmoedynamics_pa_t_kernel(tc, tokens, logits, W1, b1, g1, be1, out):
                     run_mish(1, before, mish_pool)
                     square(before, 2)
                     square(before, 3)
+                    hand_over(beat)
+                    add_bias_and_mean(chunk, 0)
+                    add_bias_and_mean(chunk, 1)
                     quantise_slots(2)
                     scale_some(2)
                     multiply_and_store(1)
@@ -600,7 +626,6 @@ def tile_softmoedynamics_pa_t_kernel(tc, tokens, logits, W1, b1, g1, be1, out):
                     multiply_block(0)
                     start_products(beat)
                     copy_block(1)
-                    add_bias_and_mean(chunk, i)
                     centre(before, 0)
                     centre(before, 1)
                     start_units(beat)
@@ -614,7 +639,6 @@ def tile_softmoedynamics_pa_t_kernel(tc, tokens, logits, W1, b1, g1, be1, out):
                     multiply_and_store(1)
                     start_products(beat)
                     copy_block(1)
-                    add_bias_and_mean(chunk, i)
                     centre(before, 2)
                     centre(before, 3)
                     scale_some(2)
@@ -623,10 +647,12 @@ def tile_softmoedynamics_pa_t_kernel(tc, tokens, logits, W1, b1, g1, be1, out):
                     start_blocks(beat)
                     copy_product(3)
                 else:
+                    hand_over(beat)
+                    add_bias_and_mean(chunk, 2)
+                    add_bias_and_mean(chunk, 3)
                     quantise_slots(2)
                     scale_some(2)
                     multiply_and_store(1)
-                    add_bias_and_mean(chunk, i)
                     multiply_block(0)
                     layer_pair(chunk + 1, 0)
                     start_products(beat)

@@ -57,9 +57,10 @@ def tile_softmoedynamics_pa_t_kernel(tc, tokens, logits, W1, b1, g1, be1, out):
         nc.vector.memset(minus_half[:], -0.5)
         eps = const.tile([P, 1], F32)
         nc.vector.memset(eps[:], 0.0)
-        nc.vector.tensor_scalar(out=eps[:], in0=eps[:], scalar1=EPS, scalar2=None, op0=ALU.add)
         warm = const.tile([P, 1], F32)
-        nc.scalar.activation(out=warm[:], in_=eps[:], func=ACT.Exp)
+        nc.vector.memset(warm[:], 0.0)
+        nc.scalar.activation(out=warm[:], in_=warm[:], func=ACT.Exp)
+        nc.vector.tensor_scalar(out=eps[:], in0=eps[:], scalar1=EPS, scalar2=None, op0=ALU.add)
 
         bias_rows = const.tile([P, E * H], BF16)
         gain_rows = const.tile([P, E * H], BF16)
@@ -195,7 +196,7 @@ def tile_softmoedynamics_pa_t_kernel(tc, tokens, logits, W1, b1, g1, be1, out):
                     products.append(handed[unit, n])
                     continue
                 if not (n == 0 and unit in made_ahead):
-                    on_scalar = n == 0 and unit >= AHEAD_UNITS or n == AGENTS - 2 and unit >= TWO_ON_SCALAR
+                    on_scalar = n == 0 and unit >= 3 * E or n == AGENTS - 2 and unit >= TWO_ON_SCALAR
                     product(bt, e, n, both, on_scalar)
                 products.append(both[:, n % 2, :])
             for n in range(parts, AGENTS):
@@ -223,7 +224,8 @@ def tile_softmoedynamics_pa_t_kernel(tc, tokens, logits, W1, b1, g1, be1, out):
                 beat, bt, e, bank = summed[0]
                 summed.remove(summed[0])
                 words = slot_pool.tile([P, P, PACK], BF16, align_bytes=64)
-                nc.scalar.copy(out=words[:], in_=bank[:].rearrange("p t b -> p b t"))
+                copy = nc.vector.tensor_copy if bt == TILES - 1 and e >= HALF else nc.scalar.copy
+                copy(out=words[:], in_=bank[:].rearrange("p t b -> p b t"))
                 copied.append((current["beat"], bt, e, words))
 
         def quantise_product(age):
@@ -552,9 +554,6 @@ def tile_softmoedynamics_pa_t_kernel(tc, tokens, logits, W1, b1, g1, be1, out):
             load_tokens(product_tiles[0])
             softmax_over_agents(raw, range(2), early, "_first")
             make_identity(nc, identity[:])
-            nc.vector.tensor_reduce(
-                out=same_batch[:], in_=identity[:].rearrange("p (g c) -> p c g", c=GROUP), axis=AX.X, op=ALU.add
-            )
             load_group(0)
             load_group(1)
             for e in range(E):
@@ -568,6 +567,10 @@ def tile_softmoedynamics_pa_t_kernel(tc, tokens, logits, W1, b1, g1, be1, out):
                     layer(0, 2)
                     layer(0, 3)
                 start_products(beat)
+                if e == 0:
+                    nc.vector.tensor_reduce(
+                        out=same_batch[:], in_=identity[:].rearrange("p (g c) -> p c g", c=GROUP), axis=AX.X, op=ALU.add
+                    )
                 if e == 1:
                     load_rows(0)
                     softmax_over_agents(raw, range(2, TILES), early, "_rest")
@@ -584,12 +587,13 @@ def tile_softmoedynamics_pa_t_kernel(tc, tokens, logits, W1, b1, g1, be1, out):
                 copy_block(1)
                 start_blocks(beat)
                 copy_product(1)
-            add_bias(0, 2)
-            add_bias(0, 3)
-            mean(0)
             for e in range(E - 2, E):
                 weights_codes(e)
             copy_product(0)
+            start_products(0)
+            add_bias(0, 2)
+            add_bias(0, 3)
+            mean(0)
             quantise_product(0)
             layer(1, 0)
             layer(1, 1)

@@ -16,6 +16,7 @@ P = 128
 B, AGENTS, E, K, H = 1024, 8, 8, 512, 512
 TILES = B // P
 PACK = 4
+RUN = 8
 GROUP = P // AGENTS
 GROUPS = P // GROUP
 EPS = 1e-5
@@ -106,7 +107,10 @@ def tile_softmoedynamics_pa_t_kernel(tc, tokens, logits, W1, b1, g1, be1, out):
 
         def weights_words(e, pool):
             rows = pool.tile([P, PACK, H], BF16)
-            nc.sync.dma_start(out=rows[:], in_=W1[e].rearrange("(p t) h -> p t h", t=PACK))
+            for t in range(PACK):
+                nc.sync.dma_start(
+                    out=rows[:, t, :], in_=W1[e].rearrange("(q t i) h -> t q i h", t=PACK, i=RUN)[t]
+                )
             words = pool.tile([P, H, PACK], BF16, align_bytes=64)
             copy = nc.vector.tensor_copy if e in (2, 5) else nc.scalar.copy
             copy(
@@ -145,8 +149,8 @@ def tile_softmoedynamics_pa_t_kernel(tc, tokens, logits, W1, b1, g1, be1, out):
         made_ahead = {}
 
         def product(bt, e, n, both, on_scalar):
-            target = both[:, n % 2, :].rearrange("b (t p) -> b t p", t=PACK)
-            source = current["tokens", bt][:, n, :].rearrange("b (p t) -> b t p", t=PACK)
+            target = both[:, n % 2, :].rearrange("b (t q i) -> b t q i", t=PACK, i=RUN)
+            source = current["tokens", bt][:, n, :].rearrange("b (q t i) -> b t q i", t=PACK, i=RUN)
             weight = disp[:, bt, n, e : e + 1]
             if on_scalar:
                 nc.scalar.activation(out=target, in_=source, func=ACT.Copy, scale=weight)
@@ -167,8 +171,8 @@ def tile_softmoedynamics_pa_t_kernel(tc, tokens, logits, W1, b1, g1, be1, out):
             nc.vector.tensor_copy(out=factor[:], in_=disp[:, bt, n, e : e + 1])
             row = gpsimd_pool.tile([P, K], F32)
             nc.gpsimd.tensor_scalar(
-                out=row[:].rearrange("b (t p) -> b t p", t=PACK),
-                in0=current["tokens", bt][:, n, :].rearrange("b (p t) -> b t p", t=PACK),
+                out=row[:].rearrange("b (t q i) -> b t q i", t=PACK, i=RUN),
+                in0=current["tokens", bt][:, n, :].rearrange("b (q t i) -> b t q i", t=PACK, i=RUN),
                 scalar1=factor[:], scalar2=0.0, op0=ALU.mult, op1=ALU.add,
             )
             handed[unit, n] = row[:]
@@ -200,11 +204,13 @@ def tile_softmoedynamics_pa_t_kernel(tc, tokens, logits, W1, b1, g1, be1, out):
                     product(bt, e, n, both, on_scalar)
                 products.append(both[:, n % 2, :])
             for n in range(parts, AGENTS):
-                target = products[n - 2].rearrange("b (t p) -> b t p", t=PACK)
-                nc.vector.scalar_tensor_tensor(
-                    out=target, in0=current["tokens", bt][:, n, :].rearrange("b (p t) -> b t p", t=PACK),
-                    scalar=disp[:, bt, n, e : e + 1], in1=target, op0=ALU.mult, op1=ALU.add,
-                )
+                target = products[n - 2].rearrange("b (t q i) -> b t q i", t=PACK, i=RUN)
+                source = current["tokens", bt][:, n, :].rearrange("b (q t i) -> b t q i", t=PACK, i=RUN)
+                for t in range(PACK):
+                    nc.vector.scalar_tensor_tensor(
+                        out=target[:, t], in0=source[:, t], scalar=disp[:, bt, n, e : e + 1], in1=target[:, t],
+                        op0=ALU.mult, op1=ALU.add,
+                    )
             if unit + 1 < AHEAD_UNITS and e + 1 < E:
                 both = sum_pool.tile([P, 2, K], F32, tag="sums")
                 product(bt, e + 1, 0, both, True)
@@ -285,8 +291,8 @@ def tile_softmoedynamics_pa_t_kernel(tc, tokens, logits, W1, b1, g1, be1, out):
                 load_group(unit + 2)
             tok32 = group_pool.tile([P, K], F32)
             nc.scalar.copy(
-                out=tok32[:].rearrange("r (t p) -> r t p", t=PACK),
-                in_=current["rows", unit][:].rearrange("r (p t) -> r t p", t=PACK),
+                out=tok32[:].rearrange("r (t q i) -> r t q i", t=PACK, i=RUN),
+                in_=current["rows", unit][:].rearrange("r (q t i) -> r t q i", t=PACK, i=RUN),
             )
             cast.append((current["beat"], g, tok32, diag, words, bt))
 

@@ -177,6 +177,9 @@ def tile_softmoedynamics_pa_t_kernel(tc, tokens, logits, W1, b1, g1, be1, out):
             )
             handed[unit, n] = row[:]
 
+        def ahead_of(unit):
+            return 2 if unit < E else 1
+
         def product_unit():
             unit = made["product"]
             if unit == E * len(product_tiles):
@@ -186,10 +189,10 @@ def tile_softmoedynamics_pa_t_kernel(tc, tokens, logits, W1, b1, g1, be1, out):
             bt = product_tiles[which]
             if e == 0:
                 new_codes(bt)
-                if which + 1 < len(product_tiles):
-                    load_tokens(product_tiles[which + 1])
+            if e == 3 and which + 1 < len(product_tiles):
+                load_tokens(product_tiles[which + 1])
             products = []
-            parts = (PARTS_FIRST if unit < E else AGENTS)
+            parts = PARTS_FIRST if unit < E else AGENTS
             for n in range(parts):
                 if n % 2 == 0:
                     if n == 0 and unit in made_ahead:
@@ -199,7 +202,7 @@ def tile_softmoedynamics_pa_t_kernel(tc, tokens, logits, W1, b1, g1, be1, out):
                 if (unit, n) in handed:
                     products.append(handed[unit, n])
                     continue
-                if not (n == 0 and unit in made_ahead):
+                if not (n < ahead_of(unit) and unit in made_ahead):
                     on_scalar = n == 0 and unit >= 3 * E or n == AGENTS - 2 and unit >= TWO_ON_SCALAR
                     product(bt, e, n, both, on_scalar)
                 products.append(both[:, n % 2, :])
@@ -213,7 +216,8 @@ def tile_softmoedynamics_pa_t_kernel(tc, tokens, logits, W1, b1, g1, be1, out):
                     )
             if unit + 1 < AHEAD_UNITS and e + 1 < E:
                 both = sum_pool.tile([P, 2, K], F32, tag="sums")
-                product(bt, e + 1, 0, both, True)
+                for n in range(ahead_of(unit + 1)):
+                    product(bt, e + 1, n, both, True)
                 made_ahead[unit + 1] = both
             bank = slot_banks.tile([P, PACK, P], F32, tag="bank")
             for t in range(PACK):
@@ -560,6 +564,10 @@ def tile_softmoedynamics_pa_t_kernel(tc, tokens, logits, W1, b1, g1, be1, out):
             load_tokens(product_tiles[0])
             softmax_over_agents(raw, range(2), early, "_first")
             make_identity(nc, identity[:])
+            both = sum_pool.tile([P, 2, K], F32, tag="sums")
+            for n in range(ahead_of(0)):
+                product(product_tiles[0], 0, n, both, True)
+            made_ahead[0] = both
             load_group(0)
             load_group(1)
             for e in range(E):
@@ -593,13 +601,12 @@ def tile_softmoedynamics_pa_t_kernel(tc, tokens, logits, W1, b1, g1, be1, out):
                 copy_block(1)
                 start_blocks(beat)
                 copy_product(1)
-            for e in range(E - 2, E):
-                weights_codes(e)
-            copy_product(0)
-            start_products(0)
             add_bias(0, 2)
             add_bias(0, 3)
             mean(0)
+            for e in range(E - 2, E):
+                weights_codes(e)
+            copy_product(0)
             quantise_product(0)
             layer(1, 0)
             layer(1, 1)

@@ -574,13 +574,13 @@ def tile_softmoedynamics_pa_t_kernel(tc, tokens, logits, W1, b1, g1, be1, out):
                 beat = e - E
                 current["beat"] = beat
                 multiply_block(0)
-                if e == HALF + 2:
-                    layer(0, 0)
-                    layer(0, 1)
                 if e == HALF + 3:
                     layer(0, 2)
                     layer(0, 3)
                 start_products(beat)
+                if e == HALF + 2:
+                    layer(0, 0)
+                    layer(0, 1)
                 if e == 0:
                     nc.vector.tensor_reduce(
                         out=same_batch[:], in_=identity[:].rearrange("p (g c) -> p c g", c=GROUP), axis=AX.X, op=ALU.add
@@ -695,12 +695,12 @@ def tile_softmoedynamics_pa_t_kernel(tc, tokens, logits, W1, b1, g1, be1, out):
 
         current["beat"] = CHUNKS * HALF
         take(mish_tanh, last - 5)
+        take(mish_tanh, last - 4)
         copy_product(0)
         quantise_slots(0)
         layer_pair(last, 2)
         add_bias(last, 0)
         add_bias(last, 1)
-        take(mish_tanh, last - 4)
         squares_of(before)
         add_bias(last, 2)
         add_bias(last, 3)

@@ -353,7 +353,7 @@ def tile_softmoedynamics_pa_t_kernel(tc, tokens, logits, W1, b1, g1, be1, out):
                 minus_mean = small.tile([P, HALF], F32)
                 group = sum(1 for end in group_ends if end <= chunk)
                 place = chunk - (group_ends[group] - MISH_GROUPS[group])
-                if group == len(MISH_GROUPS) - 1:
+                if group in (0, len(MISH_GROUPS) - 1):
                     own = small.tile([P, HALF], F32)
                     squares = own[:]
                 else:
@@ -425,6 +425,7 @@ def tile_softmoedynamics_pa_t_kernel(tc, tokens, logits, W1, b1, g1, be1, out):
             nc.scalar.activation(out=stats[:], in_=stats[:], func=ACT.Exp, scale=-0.5)
 
         to_scale = []
+        fresh = []
 
         def power(stats, chunks):
             nc.vector.tensor_scalar(out=stats, in0=stats, scalar1=1.0 / H, scalar2=EPS, op0=ALU.mult, op1=ALU.add)
@@ -617,6 +618,8 @@ def tile_softmoedynamics_pa_t_kernel(tc, tokens, logits, W1, b1, g1, be1, out):
                 beat = (chunk - 1) * HALF + i
                 current["beat"] = beat
                 if i == 0:
+                    to_scale.extend(fresh)
+                    fresh.clear()
                     square(before, 0)
                     square(before, 1)
                     multiply_block(0)
@@ -651,8 +654,6 @@ def tile_softmoedynamics_pa_t_kernel(tc, tokens, logits, W1, b1, g1, be1, out):
                 elif i == 2:
                     run_mish(1, before, mish_pool)
                     multiply_block(0)
-                    if chunk == group_ends[0]:
-                        power(statistics[0][:], members_of(0))
                     multiply_and_store(1)
                     start_products(beat)
                     copy_block(1)
@@ -664,7 +665,12 @@ def tile_softmoedynamics_pa_t_kernel(tc, tokens, logits, W1, b1, g1, be1, out):
                     start_blocks(beat)
                     copy_product(3)
                 else:
-                    hand_over(beat)
+                    if before < group_ends[0]:
+                        power(work[before]["squares"], [before])
+                        fresh.extend(to_scale)
+                        to_scale.clear()
+                    else:
+                        hand_over(beat)
                     add_bias_and_mean(chunk, 2)
                     add_bias_and_mean(chunk, 3)
                     quantise_slots(2)
@@ -687,6 +693,18 @@ def tile_softmoedynamics_pa_t_kernel(tc, tokens, logits, W1, b1, g1, be1, out):
         def squares_of(chunk):
             for i in range(HALF):
                 square(chunk, i)
+
+        def centres(chunk):
+            for i in range(HALF):
+                centre(chunk, i)
+
+        def log_of(chunk):
+            stats = work[chunk]["squares"]
+            nc.scalar.activation(out=stats, in_=stats, func=ACT.Ln, bias=eps[:], scale=1.0 / H)
+
+        def exp_of(chunk):
+            stats = work[chunk]["squares"]
+            nc.scalar.activation(out=stats, in_=stats, func=ACT.Exp, scale=-0.5)
 
         def norm(chunk):
             for i in range(HALF):
@@ -713,9 +731,12 @@ def tile_softmoedynamics_pa_t_kernel(tc, tokens, logits, W1, b1, g1, be1, out):
         square_on_vector(last, 2)
         square_on_vector(last, 3)
         scale_some(HALF)
-        norm(last)
-        multiply_and_store(1)
+        centres(last)
+        log_of(last)
         take(mish_log, last - 2)
+        exp_of(last)
+        multiply_and_store(1)
+        to_scale.extend([(last, i) for i in range(HALF)])
         scale_some(HALF)
         multiply_and_store(0)
         take(mish_tanh, last - 3)

@@ -20,6 +20,7 @@ RUN = 8
 GROUP = P // AGENTS
 GROUPS = P // GROUP
 EPS = 1e-5
+VAR_SCALE = 1.0 / H / H / H
 FLOPS = 2 * B * E * K * H + 2 * B * E * AGENTS * K
 
 BLOCK_TILES = (1, 3, 5)
@@ -392,19 +393,23 @@ def tile_softmoedynamics_pa_t_kernel(tc, tokens, logits, W1, b1, g1, be1, out):
             unused = unused_pool.tile([P, H], BF16)
             nc.scalar.activation(
                 out=unused[:], in_=work[chunk]["v"][:, i, :], func=ACT.Square,
-                bias=work[chunk]["minus_mean"][:, i : i + 1], scale=1.0, accum_out=work[chunk]["squares"][:, i : i + 1],
+                bias=work[chunk]["total"][:, i : i + 1], scale=-1.0 * H, accum_out=work[chunk]["squares"][:, i : i + 1],
             )
 
-        def square_on_vector(chunk, i):
-            both = sum_pool.tile([P, 2, K], F32, tag="sums")
-            nc.vector.tensor_scalar(
-                out=both[:, 0, :], in0=work[chunk]["v"][:, i, :], scalar1=work[chunk]["minus_mean"][:, i : i + 1],
-                scalar2=None, op0=ALU.add,
-            )
-            nc.vector.scalar_tensor_tensor(
-                out=both[:, 1, :], in0=both[:, 0, :], scalar=1.0, in1=both[:, 0, :],
-                op0=ALU.mult, op1=ALU.mult, accum_out=work[chunk]["squares"][:, i : i + 1],
-            )
+        def squares_on_vector(chunk, places):
+            tiles = []
+            for i in places:
+                both = sum_pool.tile([P, 2, K], F32, tag="sums")
+                nc.vector.tensor_scalar(
+                    out=both[:, 0, :], in0=work[chunk]["v"][:, i, :], scalar1=work[chunk]["minus_mean"][:, i : i + 1],
+                    scalar2=None, op0=ALU.add,
+                )
+                tiles.append(both)
+            for i, both in zip(places, tiles):
+                nc.vector.scalar_tensor_tensor(
+                    out=both[:, 1, :], in0=both[:, 0, :], scalar=1.0 * H * H, in1=both[:, 0, :],
+                    op0=ALU.mult, op1=ALU.mult, accum_out=work[chunk]["squares"][:, i : i + 1],
+                )
 
         def centre(chunk, i):
             v, e = work[chunk]["v"], chunk % 2 * HALF + i
@@ -418,7 +423,7 @@ def tile_softmoedynamics_pa_t_kernel(tc, tokens, logits, W1, b1, g1, be1, out):
 
         def log_variance(group, pool):
             stats = statistics[group]
-            nc.scalar.activation(out=stats[:], in_=stats[:], func=ACT.Ln, bias=eps[:], scale=1.0 / H)
+            nc.scalar.activation(out=stats[:], in_=stats[:], func=ACT.Ln, bias=eps[:], scale=VAR_SCALE)
 
         def inverse_std(group, pool):
             stats = statistics[group]
@@ -428,7 +433,7 @@ def tile_softmoedynamics_pa_t_kernel(tc, tokens, logits, W1, b1, g1, be1, out):
         fresh = []
 
         def power(stats, chunks):
-            nc.vector.tensor_scalar(out=stats, in0=stats, scalar1=1.0 / H, scalar2=EPS, op0=ALU.mult, op1=ALU.add)
+            nc.vector.tensor_scalar(out=stats, in0=stats, scalar1=VAR_SCALE, scalar2=EPS, op0=ALU.mult, op1=ALU.add)
             nc.gpsimd.tensor_tensor(out=stats, in0=stats, in1=minus_half[:, : len(chunks) * HALF], op=ALU.pow)
             to_scale.extend([(c, i) for c in chunks for i in range(HALF)])
 
@@ -625,6 +630,8 @@ def tile_softmoedynamics_pa_t_kernel(tc, tokens, logits, W1, b1, g1, be1, out):
                     multiply_block(0)
                     multiply_and_store(1)
                     start_products(beat)
+                    if chunk > 1:
+                        mean(before)
                     copy_block(1)
                     quantise_slots(2)
                     start_units(beat)
@@ -671,8 +678,8 @@ def tile_softmoedynamics_pa_t_kernel(tc, tokens, logits, W1, b1, g1, be1, out):
                         to_scale.clear()
                     else:
                         hand_over(beat)
-                    add_bias_and_mean(chunk, 2)
-                    add_bias_and_mean(chunk, 3)
+                    add_bias(chunk, 2)
+                    add_bias(chunk, 3)
                     quantise_slots(2)
                     scale_some(2)
                     multiply_and_store(1)
@@ -700,7 +707,7 @@ def tile_softmoedynamics_pa_t_kernel(tc, tokens, logits, W1, b1, g1, be1, out):
 
         def log_of(chunk):
             stats = work[chunk]["squares"]
-            nc.scalar.activation(out=stats, in_=stats, func=ACT.Ln, bias=eps[:], scale=1.0 / H)
+            nc.scalar.activation(out=stats, in_=stats, func=ACT.Ln, bias=eps[:], scale=VAR_SCALE)
 
         def exp_of(chunk):
             stats = work[chunk]["squares"]
@@ -718,6 +725,7 @@ def tile_softmoedynamics_pa_t_kernel(tc, tokens, logits, W1, b1, g1, be1, out):
         quantise_slots(0)
         layer_pair(last, 2)
         add_bias(last, 0)
+        mean(before)
         add_bias(last, 1)
         squares_of(before)
         add_bias(last, 2)
@@ -728,8 +736,7 @@ def tile_softmoedynamics_pa_t_kernel(tc, tokens, logits, W1, b1, g1, be1, out):
         square(last, 1)
         norm(before)
         take(mish_exp, last - 2)
-        square_on_vector(last, 2)
-        square_on_vector(last, 3)
+        squares_on_vector(last, (2, 3))
         scale_some(HALF)
         centres(last)
         log_of(last)

from contextlib import ExitStack

import concourse.mybir as mybir
from concourse.masks import make_identity

F32 = mybir.dt.float32
BF16 = mybir.dt.bfloat16
U32 = mybir.dt.uint32
U8 = mybir.dt.uint8
FP8X4 = mybir.dt.float8_e4m3fn_x4
ALU = mybir.AluOpType
ACT = mybir.ActivationFunctionType
AX = mybir.AxisListType

P = 128
B, AGENTS, E, K, H = 1024, 8, 8, 512, 512
TILES = B // P
PACK = 4
RUN = 8
GROUP = P // AGENTS
GROUPS = P // GROUP
EPS = 1e-5
VAR_SCALE = 1.0 / H / H / H
FLOPS = 2 * B * E * K * H + 2 * B * E * AGENTS * K

BLOCK_TILES = (1, 3, 5)
HALF = E // 2
CHUNKS = 2 * TILES
MISH_GROUPS = (2, 2, 2, 2, 2, 2, 2, 2)
PRODUCT_BEATS = [u - E for u in range(E)] + [1.7 * u for u in range(4 * E)]
BLOCK_BEATS = (
    [-6 + 0.75 * g for g in range(GROUPS)] + [2 + 1.75 * g for g in range(GROUPS)] + [18 + 1.75 * g for g in range(GROUPS)]
)
AHEAD_UNITS = 2 * E
TWO_ON_SCALAR = 4 * E
PARTS_FIRST = 6


def tile_softmoedynamics_pa_t_kernel(tc, tokens, logits, W1, b1, g1, be1, out):
    nc = tc.nc
    with ExitStack() as ctx:
        const = ctx.enter_context(tc.tile_pool(name="const", bufs=1))
        tok_pool = ctx.enter_context(tc.tile_pool(name="tok_pool", bufs=2))
        rows_pool = ctx.enter_context(tc.tile_pool(name="rows_pool", bufs=3))
        group_pool = ctx.enter_context(tc.tile_pool(name="group_pool", bufs=2))
        unused_pool = ctx.enter_context(tc.tile_pool(name="unused_pool", bufs=2))
        diag_pool = ctx.enter_context(tc.tile_pool(name="diag_pool", bufs=2))
        sum_pool = ctx.enter_context(tc.tile_pool(name="sum_pool", bufs=8))
        gpsimd_pool = ctx.enter_context(tc.tile_pool(name="gpsimd_pool", bufs=2))
        slot_pool = ctx.enter_context(tc.tile_pool(name="slot_pool", bufs=3))
        block_pool = ctx.enter_context(tc.tile_pool(name="block_pool", bufs=1))
        code_pool = ctx.enter_context(tc.tile_pool(name="code_pool", bufs=3))
        v_pool = ctx.enter_context(tc.tile_pool(name="v_pool", bufs=7))
        small = ctx.enter_context(tc.tile_pool(name="small", bufs=3))
        slot_banks = ctx.enter_context(tc.psum_pool(name="slot_banks", bufs=5))
        layer_banks = ctx.enter_context(tc.psum_pool(name="layer_banks", bufs=3))

        minus_half = const.tile([P, 2 * HALF], F32)
        nc.vector.memset(minus_half[:], -0.5)
        eps = const.tile([P, 1], F32)
        nc.vector.memset(eps[:], 0.0)
        warm = const.tile([P, 1], F32)
        nc.vector.memset(warm[:], 0.0)
        nc.scalar.activation(out=warm[:], in_=warm[:], func=ACT.Exp)
        nc.vector.tensor_scalar(out=eps[:], in0=eps[:], scalar1=EPS, scalar2=None, op0=ALU.add)

        bias_rows = const.tile([P, E * H], BF16)
        gain_rows = const.tile([P, E * H], BF16)
        shift_rows = const.tile([P, E * H], BF16)
        disp = const.tile([P, TILES, AGENTS, E], F32)
        w_codes = const.tile([P, E, H], U32, align_bytes=64)
        w_scales = const.tile([P, E, H], U8, align_bytes=64)
        identity = const.tile([P, P], F32)
        same_batch = const.tile([P, GROUP], F32)

        def load_logits(pool):
            raw = pool.tile([P, TILES, AGENTS, E], BF16)
            nc.sync.dma_start(out=raw[:], in_=logits.rearrange("(t p) n e -> p t n e", p=P))
            return raw

        def softmax_over_agents(raw, tiles, pool, tag):
            shape = [P, len(tiles), AGENTS, E]
            logit = raw[:, tiles[0] : tiles[-1] + 1]
            top = pool.tile([P, len(tiles), E], F32, tag="top" + tag)
            nc.vector.tensor_reduce(out=top[:], in_=logit.rearrange("p t n e -> p t e n"), axis=AX.X, op=ALU.max)
            ex = pool.tile(shape, F32, tag="ex" + tag)
            nc.vector.tensor_tensor(out=ex[:], in0=logit, in1=top[:].unsqueeze(2).to_broadcast(shape), op=ALU.subtract)
            flat = ex[:].rearrange("p t n e -> p (t n e)")
            nc.scalar.activation(out=flat, in_=flat, func=ACT.Exp)
            total = pool.tile([P, len(tiles), E], F32, tag="total" + tag)
            nc.vector.tensor_reduce(out=total[:], in_=ex[:].rearrange("p t n e -> p t e n"), axis=AX.X, op=ALU.add)
            inverse = pool.tile([P, len(tiles), E], F32, tag="inverse" + tag)
            nc.vector.reciprocal(out=inverse[:], in_=total[:])
            nc.vector.tensor_tensor(
                out=disp[:, tiles[0] : tiles[-1] + 1], in0=ex[:], in1=inverse[:].unsqueeze(2).to_broadcast(shape),
                op=ALU.mult,
            )

        def load_rows(half):
            cols = slice(half * HALF * H, (half + 1) * HALF * H)
            experts = slice(half * HALF, (half + 1) * HALF)
            for rows, vector in ((bias_rows, b1), (gain_rows, g1), (shift_rows, be1)):
                nc.sync.dma_start(
                    out=rows[:, cols], in_=vector[experts].rearrange("e h -> (e h)").partition_broadcast(P)
                )

        weight_words = {}

        def weights_words(e, pool):
            rows = pool.tile([P, PACK, H], BF16)
            for t in range(PACK):
                nc.sync.dma_start(
                    out=rows[:, t, :], in_=W1[e].rearrange("(q t i) h -> t q i h", t=PACK, i=RUN)[t]
                )
            words = pool.tile([P, H, PACK], BF16, align_bytes=64)
            copy = nc.vector.tensor_copy if e in (2, 5) else nc.scalar.copy
            copy(
                out=words[:].rearrange("p (c i) t -> p c t i", i=4), in_=rows[:].rearrange("p t (c i) -> p c t i", i=4)
            )
            weight_words[e] = words

        def weights_codes(e):
            nc.vector.quantize_mx(
                out=w_codes[:, e, :].bitcast(FP8X4),
                scales=w_scales[:, e, :],
                in_=weight_words[e][:].rearrange("p h t -> p (h t)"),
            )

        product_tiles = [bt for bt in range(TILES) if bt not in BLOCK_TILES]
        made = {"product": 0, "block": 0}
        current = {"beat": 0}
        slot_codes = {}
        ready = set()
        summed, copied = [], []
        grouped = []
        block_done = {}
        cast = []

        def new_codes(bt):
            codes = code_pool.tile([P, E, P], U32, align_bytes=64)
            scales = code_pool.tile([P, E, P], U8, align_bytes=64)
            slot_codes[bt] = (codes, scales)

        def load_tokens(bt):
            tok = tok_pool.tile([P, AGENTS, K], BF16)
            for pair in range(0, AGENTS, 2):
                nc.sync.dma_start(out=tok[:, pair : pair + 2], in_=tokens[bt * P : (bt + 1) * P, pair : pair + 2])
            current["tokens", bt] = tok

        made_ahead = {}

        def product(bt, e, n, both, on_scalar):
            target = both[:, n % 2, :].rearrange("b (t q i) -> b t q i", t=PACK, i=RUN)
            source = current["tokens", bt][:, n, :].rearrange("b (q t i) -> b t q i", t=PACK, i=RUN)
            weight = disp[:, bt, n, e : e + 1]
            if on_scalar:
                nc.scalar.activation(out=target, in_=source, func=ACT.Copy, scale=weight)
            else:
                nc.vector.tensor_scalar(out=target, in0=source, scalar1=weight, scalar2=None, op0=ALU.mult)

        handed = {}

        def hand_over(beat):
            unit = made["product"]
            if unit < E or unit == E * len(product_tiles) or PRODUCT_BEATS[unit] > beat + 2:
                return
            bt, e = product_tiles[unit // E], unit % E
            if ("tokens", bt) not in current:
                return
            n = 5
            factor = small.tile([P, 1], F32)
            nc.vector.tensor_copy(out=factor[:], in_=disp[:, bt, n, e : e + 1])
            row = gpsimd_pool.tile([P, K], F32)
            nc.gpsimd.tensor_scalar(
                out=row[:].rearrange("b (t q i) -> b t q i", t=PACK, i=RUN),
                in0=current["tokens", bt][:, n, :].rearrange("b (q t i) -> b t q i", t=PACK, i=RUN),
                scalar1=factor[:], scalar2=0.0, op0=ALU.mult, op1=ALU.add,
            )
            handed[unit, n] = row[:]

        def ahead_of(unit):
            return 2 if unit < E else 1

        def product_unit():
            unit = made["product"]
            if unit == E * len(product_tiles):
                return
            made["product"] = unit + 1
            which, e = divmod(unit, E)
            bt = product_tiles[which]
            if e == 0:
                new_codes(bt)
            if e == 3 and which + 1 < len(product_tiles):
                load_tokens(product_tiles[which + 1])
            products = []
            parts = PARTS_FIRST if unit < E else AGENTS
            for n in range(parts):
                if n % 2 == 0:
                    if n == 0 and unit in made_ahead:
                        both = made_ahead[unit]
                    else:
                        both = sum_pool.tile([P, 2, K], F32, tag="sums")
                if (unit, n) in handed:
                    products.append(handed[unit, n])
                    continue
                if not (n < ahead_of(unit) and unit in made_ahead):
                    on_scalar = n == 0 and unit >= 3 * E or n == AGENTS - 2 and unit >= TWO_ON_SCALAR
                    product(bt, e, n, both, on_scalar)
                products.append(both[:, n % 2, :])
            for n in range(parts, AGENTS):
                target = products[n - 2].rearrange("b (t q i) -> b t q i", t=PACK, i=RUN)
                source = current["tokens", bt][:, n, :].rearrange("b (q t i) -> b t q i", t=PACK, i=RUN)
                for t in range(PACK):
                    nc.vector.scalar_tensor_tensor(
                        out=target[:, t], in0=source[:, t], scalar=disp[:, bt, n, e : e + 1], in1=target[:, t],
                        op0=ALU.mult, op1=ALU.add,
                    )
            if unit + 1 < AHEAD_UNITS and e + 1 < E:
                both = sum_pool.tile([P, 2, K], F32, tag="sums")
                for n in range(ahead_of(unit + 1)):
                    product(bt, e + 1, n, both, True)
                made_ahead[unit + 1] = both
            bank = slot_banks.tile([P, PACK, P], F32, tag="bank")
            for t in range(PACK):
                for place in range(parts):
                    n = min(place // 4 * 4 + 3, parts - 1) - place % 4
                    nc.tensor.matmul(
                        bank[:, t, :], lhsT=products[n][:, t * P : (t + 1) * P], rhs=identity[:],
                        is_transpose=True, start=(place == 0), stop=(place == parts - 1),
                    )
            summed.append((current["beat"], bt, e, bank))

        def copy_product(age):
            while len(summed) > 0 and current["beat"] - summed[0][0] >= age:
                beat, bt, e, bank = summed[0]
                summed.remove(summed[0])
                words = slot_pool.tile([P, P, PACK], BF16, align_bytes=64)
                copy = nc.vector.tensor_copy if bt == TILES - 1 and e >= HALF else nc.scalar.copy
                copy(out=words[:], in_=bank[:].rearrange("p t b -> p b t"))
                copied.append((current["beat"], bt, e, words))

        def quantise_product(age):
            while len(copied) > 0 and current["beat"] - copied[0][0] >= age:
                beat, bt, e, words = copied[0]
                copied.remove(copied[0])
                codes, scales = slot_codes[bt]
                nc.vector.quantize_mx(
                    out=codes[:, e].bitcast(FP8X4), scales=scales[:, e], in_=words[:].rearrange("p b t -> p (b t)")
                )
                ready.add((bt, e))

        def load_group(unit):
            first = BLOCK_TILES[unit // GROUPS] * P + unit % GROUPS * GROUP
            rows = rows_pool.tile([P, K], BF16)
            nc.sync.dma_start(out=rows[:], in_=tokens[first : first + GROUP].rearrange("b n k -> (b n) k"))
            current["rows", unit] = rows

        def spread_weights(bt):
            shape = [P, E, GROUP, AGENTS]
            spread = sum_pool.tile(shape, F32, tag="sums")
            nc.vector.tensor_tensor(
                out=spread[:],
                in0=disp[:, bt].rearrange("p n e -> p e n").unsqueeze(2).to_broadcast(shape),
                in1=same_batch[:].unsqueeze(1).unsqueeze(3).to_broadcast(shape),
                op=ALU.mult,
            )
            banks = []
            for half in range(2):
                bank = slot_banks.tile([P, PACK, P], F32, tag="bank")
                for i in range(PACK):
                    nc.tensor.transpose(
                        bank[:, i, :], spread[:, half * PACK + i].rearrange("p c n -> p (c n)"), identity[:]
                    )
                banks.append(bank)
            current["spread", bt] = banks

        def copy_weights(bt):
            new_codes(bt)
            diag = diag_pool.tile([P, GROUPS, E, GROUP], F32)
            for half in range(2):
                nc.scalar.copy(
                    out=diag[:, :, half * PACK : (half + 1) * PACK, :],
                    in_=current["spread", bt][half][:].rearrange("p e (g c) -> p g e c", c=GROUP),
                )
            words = block_pool.tile([P, E, P, PACK], BF16, align_bytes=64)
            current["block", bt] = (diag, words)

        def block_unit():
            unit = made["block"]
            if unit == GROUPS * len(BLOCK_TILES):
                return
            made["block"] = unit + 1
            bt, g = BLOCK_TILES[unit // GROUPS], unit % GROUPS
            diag, words = current["block", bt]
            if unit + 2 < GROUPS * len(BLOCK_TILES):
                load_group(unit + 2)
            tok32 = group_pool.tile([P, K], F32)
            nc.scalar.copy(
                out=tok32[:].rearrange("r (t q i) -> r t q i", t=PACK, i=RUN),
                in_=current["rows", unit][:].rearrange("r (q t i) -> r t q i", t=PACK, i=RUN),
            )
            cast.append((current["beat"], g, tok32, diag, words, bt))

        def multiply_block(age):
            while len(cast) > 0 and current["beat"] - cast[0][0] >= age:
                group = cast[0]
                cast.remove(group)
                multiply_group(*group[1:])

        def multiply_group(g, tok32, diag, words, bt):
            bank = slot_banks.tile([P, PACK, P], F32, tag="bank")
            for t in range(PACK):
                nc.tensor.matmul(
                    bank[:, t, :], lhsT=tok32[:, t * P : (t + 1) * P], rhs=diag[:, g].rearrange("p e c -> p (e c)"),
                    start=True, stop=True,
                )
            grouped.append((current["beat"], g, bank, words, bt))

        def copy_block(age):
            while len(grouped) > 0 and current["beat"] - grouped[0][0] >= age:
                beat, g, bank, words, bt = grouped[0]
                grouped.remove(grouped[0])
                block_done[bt] = block_done.get(bt, 0) + 1
                nc.scalar.copy(
                    out=words[:, :, g * GROUP : (g + 1) * GROUP, :],
                    in_=bank[:].rearrange("p t (e c) -> p e c t", c=GROUP),
                )

        def quantise_block(bt, half):
            diag, words = current["block", bt]
            codes, scales = slot_codes[bt]
            assert block_done[bt] == GROUPS
            for e in range(half * HALF, (half + 1) * HALF):
                ready.add((bt, e))
            experts = slice(half * HALF, (half + 1) * HALF)
            nc.vector.quantize_mx(
                out=codes[:, experts].rearrange("p e b -> p (e b)").bitcast(FP8X4),
                scales=scales[:, experts].rearrange("p e b -> p (e b)"),
                in_=words[:, experts].rearrange("p e b t -> p (e b t)"),
            )

        work = {}
        group_ends = [sum(MISH_GROUPS[: g + 1]) for g in range(len(MISH_GROUPS))]
        statistics = {}
        finished = []

        def layer(chunk, i):
            bt, e = chunk // 2, chunk % 2 * HALF + i
            codes, scales = slot_codes[bt]
            assert (bt, e) in ready, (bt, e)
            if i == 0:
                v = v_pool.tile([P, HALF, H], F32)
                total = small.tile([P, HALF], F32)
                minus_mean = small.tile([P, HALF], F32)
                group = sum(1 for end in group_ends if end <= chunk)
                place = chunk - (group_ends[group] - MISH_GROUPS[group])
                if group in (0, len(MISH_GROUPS) - 1):
                    own = small.tile([P, HALF], F32)
                    squares = own[:]
                else:
                    if place == 0:
                        stats = small.tile([P, MISH_GROUPS[group] * HALF], F32)
                        statistics[group] = stats
                    squares = statistics[group][:, place * HALF : (place + 1) * HALF]
                work[chunk] = {"v": v, "total": total, "minus_mean": minus_mean, "squares": squares, "banks": []}
            bank = layer_banks.tile([P, H], F32)
            nc.tensor.matmul_mx(
                out=bank[:],
                lhsT=codes[:, e].bitcast(FP8X4),
                lhsT_scale=scales[:, e],
                rhs=w_codes[:, e, :].bitcast(FP8X4),
                rhs_scale=w_scales[:, e, :],
                start=True,
                stop=True,
            )
            work[chunk]["banks"].append(bank)

        def add_bias(chunk, i):
            v, total, bank = work[chunk]["v"], work[chunk]["total"], work[chunk]["banks"][i]
            e = chunk % 2 * HALF + i
            nc.vector.scalar_tensor_tensor(
                out=v[:, i, :], in0=bank[:], scalar=1.0, in1=bias_rows[:, e * H : (e + 1) * H],
                op0=ALU.mult, op1=ALU.add, accum_out=total[:, i : i + 1],
            )

        def mean(chunk):
            nc.vector.tensor_scalar(
                out=work[chunk]["minus_mean"][:], in0=work[chunk]["total"][:], scalar1=-1.0 / H, scalar2=None,
                op0=ALU.mult,
            )

        def square(chunk, i):
            unused = unused_pool.tile([P, H], BF16)
            nc.scalar.activation(
                out=unused[:], in_=work[chunk]["v"][:, i, :], func=ACT.Square,
                bias=work[chunk]["total"][:, i : i + 1], scale=-1.0 * H, accum_out=work[chunk]["squares"][:, i : i + 1],
            )

        def squares_on_vector(chunk, places):
            tiles = []
            for i in places:
                both = sum_pool.tile([P, 2, K], F32, tag="sums")
                nc.vector.tensor_scalar(
                    out=both[:, 0, :], in0=work[chunk]["v"][:, i, :], scalar1=work[chunk]["minus_mean"][:, i : i + 1],
                    scalar2=None, op0=ALU.add,
                )
                tiles.append(both)
            for i, both in zip(places, tiles):
                nc.vector.scalar_tensor_tensor(
                    out=both[:, 1, :], in0=both[:, 0, :], scalar=1.0 * H * H, in1=both[:, 0, :],
                    op0=ALU.mult, op1=ALU.mult, accum_out=work[chunk]["squares"][:, i : i + 1],
                )

        def centre(chunk, i):
            v, e = work[chunk]["v"], chunk % 2 * HALF + i
            nc.vector.scalar_tensor_tensor(
                out=v[:, i, :], in0=v[:, i, :], scalar=work[chunk]["minus_mean"][:, i : i + 1],
                in1=gain_rows[:, e * H : (e + 1) * H], op0=ALU.add, op1=ALU.mult,
            )

        def members_of(group):
            return range(group_ends[group] - MISH_GROUPS[group], group_ends[group])

        def log_variance(group, pool):
            stats = statistics[group]
            nc.scalar.activation(out=stats[:], in_=stats[:], func=ACT.Ln, bias=eps[:], scale=VAR_SCALE)

        def inverse_std(group, pool):
            stats = statistics[group]
            nc.scalar.activation(out=stats[:], in_=stats[:], func=ACT.Exp, scale=-0.5)

        to_scale = []
        fresh = []

        def power(stats, chunks):
            nc.vector.tensor_scalar(out=stats, in0=stats, scalar1=VAR_SCALE, scalar2=EPS, op0=ALU.mult, op1=ALU.add)
            nc.gpsimd.tensor_tensor(out=stats, in0=stats, in1=minus_half[:, : len(chunks) * HALF], op=ALU.pow)
            to_scale.extend([(c, i) for c in chunks for i in range(HALF)])

        def scale_some(count):
            while len(to_scale) > 0 and count > 0:
                c, i = to_scale[0]
                to_scale.remove((c, i))
                scale_and_shift(c, i)
                count -= 1

        def scale_and_shift(chunk, i):
            ready.add(("v", chunk, i))
            v, e = work[chunk]["v"], chunk % 2 * HALF + i
            nc.vector.scalar_tensor_tensor(
                out=v[:, i, :], in0=v[:, i, :], scalar=work[chunk]["squares"][:, i : i + 1],
                in1=shift_rows[:, e * H : (e + 1) * H], op0=ALU.mult, op1=ALU.add,
            )

        def flat_v(chunk):
            return work[chunk]["v"][:].rearrange("p e h -> p (e h)")

        def mish_exp(chunk, pool):
            u = pool.tile([P, HALF * H], F32)
            work[chunk]["u"] = u
            nc.scalar.activation(out=u[:], in_=flat_v(chunk), func=ACT.Exp)

        def mish_log(chunk, pool):
            u = work[chunk]["u"]
            nc.scalar.activation(out=u[:], in_=u[:], func=ACT.Ln, bias=1.0, scale=1.0)

        def mish_tanh(chunk, pool):
            u = work[chunk]["u"]
            nc.scalar.activation(out=u[:], in_=u[:], func=ACT.Tanh)
            finished.append(chunk)
            group = group_ends.index([end for end in group_ends if end > chunk][0])
            if group + 1 < len(MISH_GROUPS) - 1:
                place, size = chunk - members_of(group)[0], MISH_GROUPS[group]
                later = members_of(group + 1)
                for c in later[place * len(later) // size : (place + 1) * len(later) // size]:
                    for i in range(HALF):
                        scale_and_shift(c, i)

        def multiply_and_store(left):
            while len(finished) > left:
                chunk = finished[0]
                finished.remove(chunk)
                store(chunk)

        def store(chunk):
            u = work[chunk]["u"]
            nc.vector.tensor_tensor(out=u[:], in0=flat_v(chunk), in1=u[:], op=ALU.mult)
            bt, first = chunk // 2, chunk % 2 * HALF
            rows = out[bt * P : (bt + 1) * P, first : first + HALF].rearrange("b e h -> b (e h)")
            nc.sync.dma_start(out=rows, in_=u[:])

        def finish_in_pieces(chunk):
            u, v = work[chunk]["u"], work[chunk]["v"]
            bt, first = chunk // 2, chunk % 2 * HALF
            for i in range(HALF):
                nc.scalar.activation(out=u[:, i * H : (i + 1) * H], in_=u[:, i * H : (i + 1) * H], func=ACT.Tanh)
                nc.vector.tensor_tensor(
                    out=u[:, i * H : (i + 1) * H], in0=v[:, i, :], in1=u[:, i * H : (i + 1) * H], op=ALU.mult
                )
                nc.sync.dma_start(
                    out=out[bt * P : (bt + 1) * P, first + i], in_=u[:, i * H : (i + 1) * H]
                )

        mish_queue = []

        for group in range(len(MISH_GROUPS)):
            if 0 < group < len(MISH_GROUPS) - 1:
                mish_queue.append((log_variance, group))
                mish_queue.append((inverse_std, group))
            if group > 0:
                mish_queue.extend([(mish_tanh, c) for c in members_of(group - 1)])
            mish_queue.extend([(mish_exp, c) for c in members_of(group)])
            mish_queue.extend([(mish_log, c) for c in members_of(group)])
        mish_queue.extend([(mish_tanh, c) for c in members_of(len(MISH_GROUPS) - 1)])

        def run_mish(count, squared, pool):
            while len(mish_queue) > 0 and count > 0:
                stage, what = mish_queue[0]
                if stage == log_variance and group_ends[what] > squared:
                    return
                if stage == mish_exp and ("v", what, HALF - 1) not in ready:
                    return
                mish_queue.remove(mish_queue[0])
                stage(what, pool)
                if stage not in (log_variance, inverse_std):
                    count -= 1

        pinned = {mybir.EngineType.PE, mybir.EngineType.DVE, mybir.EngineType.Activation}
        ctx.enter_context(tc.manual_schedule(engines=pinned))

        def add_bias_and_mean(chunk, i):
            if chunk < CHUNKS:
                add_bias(chunk, i)
                if i == HALF - 1:
                    mean(chunk)

        def layer_pair(chunk, first):
            if chunk < CHUNKS:
                layer(chunk, first)
                layer(chunk, first + 1)

        def quantise_slots(age):
            quantise_product(age)
            finish_blocks()

        def start_units(beat):
            for bt in BLOCK_TILES:
                first = BLOCK_BEATS[BLOCK_TILES.index(bt) * GROUPS]
                if int(first) - 2 == beat:
                    spread_weights(bt)
                if int(first) - 1 == beat:
                    copy_weights(bt)

        def start_products(beat):
            while made["product"] < len(PRODUCT_BEATS) and PRODUCT_BEATS[made["product"]] <= beat:
                product_unit()

        def start_blocks(beat):
            while made["block"] < len(BLOCK_BEATS) and BLOCK_BEATS[made["block"]] <= beat:
                block_unit()

        def finish_blocks():
            for bt in BLOCK_TILES:
                if block_done.get(bt, 0) == GROUPS and (bt, 0) not in ready:
                    quantise_block(bt, 0)
                    quantise_block(bt, 1)

        with tc.tile_pool(name="early", bufs=1) as early, tc.tile_pool(name="staging", bufs=4) as staging:
            raw = load_logits(early)
            load_tokens(product_tiles[0])
            softmax_over_agents(raw, range(2), early, "_first")
            make_identity(nc, identity[:])
            both = sum_pool.tile([P, 2, K], F32, tag="sums")
            for n in range(ahead_of(0)):
                product(product_tiles[0], 0, n, both, True)
            made_ahead[0] = both
            load_group(0)
            load_group(1)
            for e in range(E):
                beat = e - E
                current["beat"] = beat
                multiply_block(0)
                if e == HALF + 3:
                    layer(0, 2)
                    layer(0, 3)
                start_products(beat)
                if e == HALF + 2:
                    layer(0, 0)
                    layer(0, 1)
                if e == 0:
                    nc.vector.tensor_reduce(
                        out=same_batch[:], in_=identity[:].rearrange("p (g c) -> p c g", c=GROUP), axis=AX.X, op=ALU.add
                    )
                if e == 1:
                    load_rows(0)
                    softmax_over_agents(raw, range(2, TILES), early, "_rest")
                start_units(beat)
                if e >= 2:
                    weights_codes(e - 2)
                quantise_product(1)
                if e == 5:
                    load_rows(1)
                if e == HALF + 3:
                    add_bias(0, 0)
                    add_bias(0, 1)
                weights_words(e, staging)
                copy_block(1)
                start_blocks(beat)
                copy_product(1)
            add_bias(0, 2)
            add_bias(0, 3)
            mean(0)
            for e in range(E - 2, E):
                weights_codes(e)
            copy_product(0)
            quantise_product(0)
            layer(1, 0)
            layer(1, 1)
        mish_pool = ctx.enter_context(tc.tile_pool(name="mish_pool", bufs=5))
        for chunk in range(1, CHUNKS - 1):
            before = chunk - 1
            for i in range(HALF):
                beat = (chunk - 1) * HALF + i
                current["beat"] = beat
                if i == 0:
                    to_scale.extend(fresh)
                    fresh.clear()
                    square(before, 0)
                    square(before, 1)
                    multiply_block(0)
                    multiply_and_store(1)
                    start_products(beat)
                    if chunk > 1:
                        mean(before)
                    copy_block(1)
                    quantise_slots(2)
                    start_units(beat)
                    start_blocks(beat)
                    run_mish(1, before, mish_pool)
                    copy_product(3)
                    scale_some(2)
                elif i == 1:
                    run_mish(1, before, mish_pool)
                    square(before, 2)
                    square(before, 3)
                    hand_over(beat)
                    add_bias_and_mean(chunk, 0)
                    add_bias_and_mean(chunk, 1)
                    quantise_slots(2)
                    scale_some(2)
                    multiply_and_store(1)
                    layer_pair(chunk, 2)
                    multiply_block(0)
                    start_products(beat)
                    copy_block(1)
                    centre(before, 0)
                    centre(before, 1)
                    start_units(beat)
                    start_blocks(beat)
                    copy_product(3)
                elif i == 2:
                    run_mish(1, before, mish_pool)
                    multiply_block(0)
                    multiply_and_store(1)
                    start_products(beat)
                    copy_block(1)
                    centre(before, 2)
                    centre(before, 3)
                    scale_some(2)
                    quantise_slots(2)
                    start_units(beat)
                    start_blocks(beat)
                    copy_product(3)
                else:
                    if before < group_ends[0]:
                        power(work[before]["squares"], [before])
                        fresh.extend(to_scale)
                        to_scale.clear()
                    else:
                        hand_over(beat)
                    add_bias(chunk, 2)
                    add_bias(chunk, 3)
                    quantise_slots(2)
                    scale_some(2)
                    multiply_and_store(1)
                    multiply_block(0)
                    layer_pair(chunk + 1, 0)
                    start_products(beat)
                    start_units(beat)
                    start_blocks(beat)
                    run_mish(1, chunk, mish_pool)
                    copy_block(1)
                    copy_product(3)
        last, before = CHUNKS - 1, CHUNKS - 2

        def take(stage, chunk):
            while (stage, chunk) in mish_queue:
                run_mish(1, CHUNKS, mish_pool)

        def squares_of(chunk):
            for i in range(HALF):
                square(chunk, i)

        def centres(chunk):
            for i in range(HALF):
                centre(chunk, i)

        def log_of(chunk):
            stats = work[chunk]["squares"]
            nc.scalar.activation(out=stats, in_=stats, func=ACT.Ln, bias=eps[:], scale=VAR_SCALE)

        def exp_of(chunk):
            stats = work[chunk]["squares"]
            nc.scalar.activation(out=stats, in_=stats, func=ACT.Exp, scale=-0.5)

        def norm(chunk):
            for i in range(HALF):
                centre(chunk, i)
            power(work[chunk]["squares"], [chunk])

        current["beat"] = CHUNKS * HALF
        take(mish_tanh, last - 5)
        take(mish_tanh, last - 4)
        copy_product(0)
        quantise_slots(0)
        layer_pair(last, 2)
        add_bias(last, 0)
        mean(before)
        add_bias(last, 1)
        squares_of(before)
        add_bias(last, 2)
        add_bias(last, 3)
        mean(last)
        take(mish_exp, last - 3)
        square(last, 0)
        square(last, 1)
        norm(before)
        take(mish_exp, last - 2)
        squares_on_vector(last, (2, 3))
        scale_some(HALF)
        centres(last)
        log_of(last)
        take(mish_log, last - 2)
        exp_of(last)
        multiply_and_store(1)
        to_scale.extend([(last, i) for i in range(HALF)])
        scale_some(HALF)
        multiply_and_store(0)
        take(mish_tanh, last - 3)
        multiply_and_store(0)
        take(mish_tanh, last - 2)
        take(mish_log, last)
        multiply_and_store(0)
        for chunk in (before, last):
            finish_in_pieces(chunk)
